import numpy as np
import ml_dtypes


def mxq(x, axis, fmt="e4m3"):
    dtype, down = {"e4m3": (ml_dtypes.float8_e4m3fn, 7), "e5m2": (ml_dtypes.float8_e5m2, 14)}[fmt]
    v = np.moveaxis(np.asarray(x, np.float32).astype(ml_dtypes.bfloat16).astype(np.float64), axis, -1)
    blocks = v.reshape(v.shape[:-1] + (-1, 32))
    amax = np.abs(blocks).max(-1, keepdims=True)
    byte = np.maximum(np.where(amax > 0, np.frexp(amax)[1] - 1 + 127, 0) - down, 1)
    scale = np.exp2(byte - 127.0)
    codes = (blocks / scale).astype(np.float32).astype(dtype).astype(np.float64)
    return np.moveaxis((codes * scale).reshape(v.shape), -1, axis)


WIDE = False


def mx_kscale(k):
    if not WIDE:
        return np.ones(k)
    levels = np.array([10, -10, 5, -5, 0])
    a = np.random.permutation(np.resize(levels, k // 512 * 4)).reshape(k // 512, 4)
    idx = np.arange(k)
    return np.exp2(a[idx // 512, idx % 128 // 32])


BF16 = ml_dtypes.bfloat16


def bf(x):
    return np.asarray(x, np.float32).astype(BF16)


def f64(x):
    return np.asarray(x).astype(np.float64)


E2M1 = np.array([0.0, 0.5, 1.0, 1.5, 2.0, 3.0, 4.0, 6.0, -0.0, -0.5, -1.0, -1.5, -2.0, -3.0, -4.0, -6.0])


def pack_weight(w, fmt):
    k, n = w.shape
    w = f64(bf(w)).reshape(k // 32, 32, n)
    amax = np.abs(w).max(1)
    if fmt == "e4m3":
        byte = np.frexp(amax)[1] - 1 + 127 - 7
    else:
        mant, ex = np.frexp(amax / 6.0)
        byte = np.where(mant > 0.5, ex, ex - 1) + 127
    byte = np.clip(np.where(amax > 0, byte, 1), 1, 254)
    scaled = (w * np.exp2(127.0 - byte)[:, None, :]).reshape(k, n).astype(np.float32)
    by_word = np.ascontiguousarray(scaled.reshape(k // 512, 128, 4, n).transpose(0, 1, 3, 2))
    if fmt == "e4m3":
        words = by_word.astype(ml_dtypes.float8_e4m3fn).view(np.uint8)
    else:
        c = by_word.astype(ml_dtypes.float4_e2m1fn).view(np.uint8) & 0xF
        words = c[..., 0::2] | (c[..., 1::2] << 4)
    return np.ascontiguousarray(words), np.ascontiguousarray(byte.astype(np.uint8).reshape(k // 512, 16, n))


def unpack_weight(words, scales, fmt):
    g, p, n, _ = words.shape
    if fmt == "e4m3":
        vals = np.ascontiguousarray(words).view(ml_dtypes.float8_e4m3fn).astype(np.float64)
    else:
        nib = np.empty((g, p, n, 4), np.uint8)
        nib[..., 0::2] = words & 0xF
        nib[..., 1::2] = words >> 4
        vals = E2M1[nib]
    vals = vals * np.repeat(np.exp2(scales.astype(np.float64) - 127.0), 8, axis=1)[..., None]
    return vals.transpose(0, 1, 3, 2).reshape(g * 512, n)


B, S, I, Hd = 4, 32, 128, 2048


def sigmoid(v):
    return 1.0 / (1.0 + np.exp(-v))


def setup_inputs():
    t = mx_kscale(Hd)
    x = bf(np.random.standard_normal((B, S, I)))
    w_emb = bf(np.random.standard_normal((Hd, I)) / np.sqrt(I) * t[:, None])
    b_emb = bf(np.random.standard_normal(Hd) * 0.5 * t)
    w_ih = np.random.standard_normal((3 * Hd, Hd)) / np.sqrt(Hd) / t[None, :]
    w_ih_words, w_ih_scales = pack_weight(np.ascontiguousarray(w_ih.T), "e4m3")
    b_ih = bf(np.random.standard_normal(3 * Hd) * 0.5)
    b_hh = bf(np.random.standard_normal(3 * Hd))
    return {"x": x,
            "w_emb": w_emb,
            "b_emb": b_emb,
            "w_ih_words": w_ih_words,
            "w_ih_scales": w_ih_scales,
            "b_ih": b_ih,
            "b_hh": b_hh}


def reference(x, w_emb, b_emb, w_ih_words, w_ih_scales, b_ih, b_hh):
    emb = f64(x) @ f64(w_emb).T + f64(b_emb)
    gi = (mxq(emb, 2, "e4m3") @ unpack_weight(w_ih_words, w_ih_scales, "e4m3")) + f64(b_ih)
    ir, iz, inn = np.split(gi, 3, axis=-1)
    b_hr, b_hz, b_hn = np.split(f64(b_hh), 3)
    r = sigmoid(ir + b_hr)
    z = sigmoid(iz + b_hz)
    n = np.tanh(inn + r * b_hn)
    h = (1.0 - z) * n
    H = h[:, :-1, :]
    h_last = h[:, -1, :][None]
    return (H, h_last)

@@ -1,0 +1,199 @@
+from contextlib import ExitStack
+
+import concourse.mybir as mybir
+from concourse.masks import make_identity
+
+F32 = mybir.dt.float32
+BF16 = mybir.dt.bfloat16
+I32 = mybir.dt.int32
+U32 = mybir.dt.uint32
+U8 = mybir.dt.uint8
+FP8X4 = mybir.dt.float8_e4m3fn_x4
+ACT = mybir.ActivationFunctionType
+ALU = mybir.AluOpType
+
+P = 128
+HID = 2048
+GROUPS = 4
+NT = HID // P
+FLOPS = 2 * 128 * 128 * 2048 + 2 * 128 * 2048 * 6144
+
+GATE_OFF = {"r": 0, "z": HID, "n": 2 * HID}
+CHUNKS = [
+    ("r", 0, 2048, True),
+    ("n", 0, 1024, False),
+    ("n", 1024, 1024, False),
+    ("z", 0, 1024, False),
+    ("z", 1024, 512, False),
+    ("z", 1536, 256, False),
+    ("z", 1792, 256, False),
+]
+STORE_ROWS = [(0, 64), (64, 96), (96, 112), (112, 120), (120, 124)]
+
+
+def tile_encoderrnn_w_kernel(tc, x, w_emb, b_emb, w_ih_words, w_ih_scales, b_ih, b_hh, out_0, out_1):
+    nc = tc.nc
+    with ExitStack() as ctx:
+        keep = ctx.enter_context(tc.tile_pool(name="keep", bufs=1))
+        work = ctx.enter_context(tc.tile_pool(name="work", bufs=4))
+        psum = ctx.enter_context(tc.psum_pool(name="psum", bufs=1))
+
+        planes = keep.tile([P, 3 * HID], U8, name="planes", align_bytes=64)
+        nc.vector.memset(planes[:].bitcast(I32), 0)
+        warm = keep.tile([P, 1], F32, name="warm")
+        nc.vector.memset(warm[:], 0.0)
+        warm2 = keep.tile([P, 1], F32, name="warm2")
+        nc.scalar.activation(out=warm2[:], in_=warm[:], func=ACT.Sigmoid)
+
+        x_sb = keep.tile([P, P], BF16, name="x_sb")
+        nc.sync.dma_start(out=x_sb[:], in_=x.rearrange("b s i -> (b s) i"))
+        w_sb = keep.tile([P, 16, P], BF16, name="w_sb")
+        nc.sync.dma_start(
+            out=w_sb[:].rearrange("p (g t) i -> p g (t i)", t=4),
+            in_=w_emb.rearrange("(g p t) i -> p g (t i)", g=GROUPS, p=P, t=4),
+        )
+        be_sb = keep.tile([P, 16], BF16, name="be_sb")
+        nc.scalar.dma_start(
+            out=be_sb[:].rearrange("p (g t) -> p g t", t=4),
+            in_=b_emb.rearrange("(g p t) -> p g t", g=GROUPS, p=P, t=4),
+        )
+        brow = keep.tile([P, P], BF16, name="brow")
+        nc.vector.memset(brow[:], 0.0)
+        nc.scalar.dma_start(out=brow[0:48, :], in_=b_ih.rearrange("(r c) -> r c", c=P))
+        nc.scalar.dma_start(out=brow[48:96, :], in_=b_hh.rearrange("(r c) -> r c", c=P))
+
+        sc32 = w_ih_scales.bitcast(I32)
+        for q in range(4):
+            nc.sync.dma_start(
+                out=planes[32 * q : 32 * q + 16, :].bitcast(I32),
+                in_=sc32[:, 4 * q : 4 * q + 4, :],
+            )
+
+        w32 = w_ih_words.rearrange("g p n t -> g p (n t)").bitcast(I32)
+        wtiles = []
+        for ci, (gate, c0, cols, by_group) in enumerate(CHUNKS):
+            wt = keep.tile([P, GROUPS, cols], I32, name="wt%d" % ci, align_bytes=64)
+            n0 = GATE_OFF[gate] + c0
+            if by_group:
+                for g in range(GROUPS):
+                    nc.sync.dma_start(out=wt[:, g, :], in_=w32[g, :, n0 : n0 + cols])
+            else:
+                nc.sync.dma_start(out=wt[:], in_=w32[:, :, n0 : n0 + cols].rearrange("g p n -> p g n"))
+            wtiles.append(wt)
+
+        ident_bf = keep.tile([P, P], BF16, name="ident_bf")
+        make_identity(nc, ident_bf[:])
+        ident_f = keep.tile([P, P], F32, name="ident_f")
+        make_identity(nc, ident_f[:])
+        perm = keep.tile([P, P], BF16, name="perm")
+        nc.vector.tensor_copy(
+            out=perm[:, 0:124].rearrange("p (b s) -> p b s", s=31),
+            in_=ident_bf[:].rearrange("p (b s) -> p b s", s=32)[:, :, 0:31],
+        )
+        nc.vector.tensor_copy(out=perm[:, 124:128], in_=ident_bf[:, 31:128:32])
+
+        xb_ps = psum.tile([P, 2, P], BF16, name="xb_ps", tag="tr", bufs=2)
+        nc.tensor.transpose(xb_ps[:, 0, :], x_sb[:], perm[:])
+        nc.tensor.transpose(xb_ps[:, 1, :], brow[:], ident_bf[:])
+        xT = keep.tile([P, P], BF16, name="xT")
+        nc.vector.tensor_copy(out=xT[:], in_=xb_ps[:, 0, :])
+        bT = keep.tile([P, P], F32, name="bT")
+        nc.vector.tensor_copy(out=bT[:], in_=xb_ps[:, 1, :])
+
+        wT = keep.tile([P, 16, P], BF16, name="wT")
+        for h in range(2):
+            wT_ps = psum.tile([P, 8, P], BF16, name="wT_ps", tag="acc", bufs=6)
+            for q in range(8):
+                nc.tensor.transpose(wT_ps[:, q, :], w_sb[:, 8 * h + q, :], ident_bf[:])
+            if h == 0:
+                nc.vector.tensor_copy(out=wT[:, 0:8, :], in_=wT_ps[:])
+            else:
+                nc.scalar.copy(out=wT[:, 8:16, :], in_=wT_ps[:])
+
+        brz = keep.tile([P, 32], F32, name="brz")
+        nc.vector.tensor_tensor(out=brz[:], in0=bT[:, 0:32], in1=bT[:, 48:80], op=ALU.add)
+        bzn = keep.tile([P, 16], F32, name="bzn")
+        nc.vector.tensor_scalar(out=bzn[:], in0=brz[:, 16:32], scalar1=-1.0, scalar2=None, op0=ALU.mult)
+
+        grouped = keep.tile([P, GROUPS, P, 4], BF16, name="grouped", align_bytes=64)
+        for g in range(GROUPS):
+            e_ps = psum.tile([P, 4, P], F32, name="e_ps", tag="acc", bufs=6)
+            for t in range(4):
+                nc.tensor.matmul(e_ps[:, t, :], lhsT=wT[:, 4 * g + t, :], rhs=xT[:], start=True, stop=True)
+            nc.vector.tensor_tensor(
+                out=grouped[:, g, :, :],
+                in0=e_ps[:].rearrange("p t k -> p k t"),
+                in1=be_sb[:, 4 * g : 4 * g + 4].unsqueeze(1).to_broadcast([P, P, 4]),
+                op=ALU.add,
+            )
+        ecodes = keep.tile([P, GROUPS * P], U32, name="ecodes", align_bytes=64)
+        eplane = keep.tile([P, GROUPS * P], U8, name="eplane", align_bytes=64)
+        nc.vector.quantize_mx(
+            out=ecodes[:].bitcast(FP8X4),
+            scales=eplane[:],
+            in_=grouped[:].rearrange("p g k t -> p (g k t)"),
+        )
+
+        def passes(wt, lc, n0):
+            acc = psum.tile([P, P], F32, name="acc", tag="acc", bufs=6)
+            for g in range(GROUPS):
+                nc.tensor.matmul_mx(
+                    out=acc[:],
+                    lhsT=wt[:, g, lc : lc + P].bitcast(FP8X4),
+                    lhsT_scale=planes[4 * g : P, n0 : n0 + P],
+                    rhs=ecodes[:, g * P : (g + 1) * P].bitcast(FP8X4),
+                    rhs_scale=eplane[:, g * P : (g + 1) * P],
+                    start=(g == 0),
+                    stop=(g == GROUPS - 1),
+                )
+            return acc
+
+        out_h = out_0.rearrange("b s j -> (b s) j")
+        out_l = out_1.rearrange("o b j -> (o b) j")
+        r_t = {}
+        n_t = {}
+
+        def finish(c0, hts):
+            width = P * len(hts)
+            tr = psum.tile([P, width], F32, name="tr", tag="tr", bufs=2)
+            for q, ht in enumerate(hts):
+                nc.tensor.transpose(tr[:, q * P : (q + 1) * P], ht[:], ident_f[:])
+            o_sb = work.tile([P, width], F32, name="o_sb", tag="o_sb%d" % width)
+            nc.vector.tensor_copy(out=o_sb[:], in_=tr[:])
+            for p0, p1 in STORE_ROWS:
+                nc.sync.dma_start(out=out_h[p0:p1, c0 : c0 + width], in_=o_sb[p0:p1, :])
+            nc.sync.dma_start(out=out_l[:, c0 : c0 + width], in_=o_sb[124:128, :])
+
+        pending = []
+        for ci, (gate, c0, cols, by_group) in enumerate(CHUNKS):
+            wt = wtiles[ci]
+            for s0 in range(0, cols, 512):
+                sub = min(512, cols - s0)
+                hts = []
+                for lc in range(s0, s0 + sub, P):
+                    j = (c0 + lc) // P
+                    acc = passes(wt, lc, GATE_OFF[gate] + c0 + lc)
+                    if gate == "r":
+                        r_j = keep.tile([P, P], F32, name="r%d" % j)
+                        nc.scalar.activation(out=r_j[:], in_=acc[:], func=ACT.Sigmoid, bias=brz[:, j : j + 1], scale=1.0)
+                        r_t[j] = r_j
+                    elif gate == "n":
+                        u = work.tile([P, P], F32, name="u")
+                        nc.vector.scalar_tensor_tensor(
+                            out=u[:], in0=r_t[j][:], scalar=bT[:, 80 + j : 81 + j], in1=acc[:], op0=ALU.mult, op1=ALU.add
+                        )
+                        n_j = keep.tile([P, P], F32, name="n%d" % j)
+                        nc.scalar.activation(out=n_j[:], in_=u[:], func=ACT.Tanh, bias=bT[:, 32 + j : 33 + j], scale=1.0)
+                        n_t[j] = n_j
+                    else:
+                        zc = work.tile([P, P], F32, name="zc")
+                        nc.scalar.activation(out=zc[:], in_=acc[:], func=ACT.Sigmoid, bias=bzn[:, j : j + 1], scale=-1.0)
+                        ht = work.tile([P, P], F32, name="ht", bufs=8)
+                        nc.vector.tensor_tensor(out=ht[:], in0=zc[:], in1=n_t[j][:], op=ALU.mult)
+                        hts.append(ht)
+                if gate == "z":
+                    for args in pending:
+                        finish(args[0], args[1])
+                    pending = [(c0 + s0, hts)]
+        for args in pending:
+            finish(args[0], args[1])

@@ -28,7 +28,16 @@ CHUNKS = [
     ("z", 1536, 256, False),
     ("z", 1792, 256, False),
 ]
-STORE_ROWS = [(0, 64), (64, 96), (96, 112), (112, 120), (120, 124)]
+STORE_SETS = [(0, 128, 2, 0, 64), (1, 128, 4, 64, 32), (3, 67, 4, 96, 16), (67, 99, 4, 112, 8), (99, 115, 4, 120, 4)]
+PERM_COPIES = [
+    (0, 62, 2, 0, 31, 1),
+    (62, 124, 2, 32, 63, 1),
+    (124, 128, 2, 64, 66, 1),
+    (1, 117, 4, 66, 95, 1),
+    (117, 128, 4, 96, 99, 1),
+    (3, 115, 4, 99, 127, 1),
+    (115, 128, 4, 31, 128, 32),
+]
 
 
 def tile_encoderrnn_w_kernel(tc, x, w_emb, b_emb, w_ih_words, w_ih_scales, b_ih, b_hh, out_0, out_1):
@@ -86,11 +95,8 @@ def tile_encoderrnn_w_kernel(tc, x, w_emb, b_emb, w_ih_words, w_ih_scales, b_ih,
         ident_f = keep.tile([P, P], F32, name="ident_f")
         make_identity(nc, ident_f[:])
         perm = keep.tile([P, P], BF16, name="perm")
-        nc.vector.tensor_copy(
-            out=perm[:, 0:124].rearrange("p (b s) -> p b s", s=31),
-            in_=ident_bf[:].rearrange("p (b s) -> p b s", s=32)[:, :, 0:31],
-        )
-        nc.vector.tensor_copy(out=perm[:, 124:128], in_=ident_bf[:, 31:128:32])
+        for d0, d1, ds, s0, s1, ss in PERM_COPIES:
+            nc.vector.tensor_copy(out=perm[:, d0:d1:ds], in_=ident_bf[:, s0:s1:ss])
 
         xb_ps = psum.tile([P, 2, P], BF16, name="xb_ps", tag="tr", bufs=2)
         nc.tensor.transpose(xb_ps[:, 0, :], x_sb[:], perm[:])
@@ -160,9 +166,9 @@ def tile_encoderrnn_w_kernel(tc, x, w_emb, b_emb, w_ih_words, w_ih_scales, b_ih,
                 nc.tensor.transpose(tr[:, q * P : (q + 1) * P], ht[:], ident_f[:])
             o_sb = work.tile([P, width], F32, name="o_sb", tag="o_sb%d" % width)
             nc.vector.tensor_copy(out=o_sb[:], in_=tr[:])
-            for p0, p1 in STORE_ROWS:
-                nc.sync.dma_start(out=out_h[p0:p1, c0 : c0 + width], in_=o_sb[p0:p1, :])
-            nc.sync.dma_start(out=out_l[:, c0 : c0 + width], in_=o_sb[124:128, :])
+            for p0, p1, ps, r0, rows in STORE_SETS:
+                nc.sync.dma_start(out=out_h[r0 : r0 + rows, c0 : c0 + width], in_=o_sb[p0:p1:ps, :])
+            nc.sync.dma_start(out=out_l[:, c0 : c0 + width], in_=o_sb[115:128:4, :])
 
         pending = []
         for ci, (gate, c0, cols, by_group) in enumerate(CHUNKS):

@@ -28,6 +28,7 @@ CHUNKS = [
     ("z", 1536, 256, False),
     ("z", 1792, 256, False),
 ]
+STORE_GROUPS = [(0, 1024), (1024, 512), (1536, 512)]
 STORE_SETS = [(0, 128, 2, 0, 64), (1, 128, 4, 64, 32), (3, 67, 4, 96, 16), (67, 99, 4, 112, 8), (99, 115, 4, 120, 4)]
 PERM_COPIES = [
     (0, 62, 2, 0, 31, 1),
@@ -159,16 +160,23 @@ def tile_encoderrnn_w_kernel(tc, x, w_emb, b_emb, w_ih_words, w_ih_scales, b_ih,
         r_t = {}
         n_t = {}
 
+        o_tiles = {}
+        for gi, (g0, gw) in enumerate(STORE_GROUPS):
+            o_tiles[gi] = keep.tile([P, gw], F32, name="o_sb%d" % gi)
+
         def finish(c0, hts):
             width = P * len(hts)
             tr = psum.tile([P, width], F32, name="tr", tag="tr", bufs=2)
             for q, ht in enumerate(hts):
                 nc.tensor.transpose(tr[:, q * P : (q + 1) * P], ht[:], ident_f[:])
-            o_sb = work.tile([P, width], F32, name="o_sb", tag="o_sb%d" % width)
-            nc.vector.tensor_copy(out=o_sb[:], in_=tr[:])
-            for p0, p1, ps, r0, rows in STORE_SETS:
-                nc.sync.dma_start(out=out_h[r0 : r0 + rows, c0 : c0 + width], in_=o_sb[p0:p1:ps, :])
-            nc.sync.dma_start(out=out_l[:, c0 : c0 + width], in_=o_sb[115:128:4, :])
+            for gi, (g0, gw) in enumerate(STORE_GROUPS):
+                if g0 <= c0 < g0 + gw:
+                    o_sb = o_tiles[gi]
+                    nc.vector.tensor_copy(out=o_sb[:, c0 - g0 : c0 - g0 + width], in_=tr[:])
+                    if c0 + width == g0 + gw:
+                        for p0, p1, ps, r0, rows in STORE_SETS:
+                            nc.sync.dma_start(out=out_h[r0 : r0 + rows, g0 : g0 + gw], in_=o_sb[p0:p1:ps, :])
+                        nc.sync.dma_start(out=out_l[:, g0 : g0 + gw], in_=o_sb[115:128:4, :])
 
         pending = []
         for ci, (gate, c0, cols, by_group) in enumerate(CHUNKS):

@@ -15,18 +15,24 @@ ALU = mybir.AluOpType
 P = 128
 HID = 2048
 GROUPS = 4
-NT = HID // P
+BANK = 512
+NB = HID // BANK
 FLOPS = 2 * 128 * 128 * 2048 + 2 * 128 * 2048 * 6144
 
 GATE_OFF = {"r": 0, "z": HID, "n": 2 * HID}
-CHUNKS = [
-    ("r", 0, 2048, True),
-    ("n", 0, 1024, False),
-    ("n", 1024, 1024, False),
-    ("z", 0, 1024, False),
-    ("z", 1024, 512, False),
-    ("z", 1536, 256, False),
-    ("z", 1792, 256, False),
+LOADS = [
+    ("r", 0, 1, 0, 2048),
+    ("r", 1, 1, 0, 2048),
+    ("r", 2, 1, 0, 2048),
+    ("r", 3, 1, 0, 2048),
+    ("n", 0, 1, 0, 2048),
+    ("n", 1, 1, 0, 2048),
+    ("n", 2, 1, 0, 2048),
+    ("n", 3, 1, 0, 2048),
+    ("z", 0, 4, 0, 1024),
+    ("z", 0, 4, 1024, 512),
+    ("z", 0, 3, 1536, 512),
+    ("z", 3, 1, 1536, 512),
 ]
 STORE_GROUPS = [(0, 1024), (1024, 512), (1536, 512)]
 STORE_SETS = [(0, 128, 2, 0, 64), (1, 128, 4, 64, 32), (3, 67, 4, 96, 16), (67, 99, 4, 112, 8), (99, 115, 4, 120, 4)]
@@ -45,8 +51,8 @@ def tile_encoderrnn_w_kernel(tc, x, w_emb, b_emb, w_ih_words, w_ih_scales, b_ih,
     nc = tc.nc
     with ExitStack() as ctx:
         keep = ctx.enter_context(tc.tile_pool(name="keep", bufs=1))
-        work = ctx.enter_context(tc.tile_pool(name="work", bufs=4))
-        psum = ctx.enter_context(tc.psum_pool(name="psum", bufs=1))
+        work = ctx.enter_context(tc.tile_pool(name="work", bufs=3))
+        psum = ctx.enter_context(tc.psum_pool(name="psum", bufs=8))
 
         planes = keep.tile([P, 3 * HID], U8, name="planes", align_bytes=64)
         nc.vector.memset(planes[:].bitcast(I32), 0)
@@ -81,14 +87,10 @@ def tile_encoderrnn_w_kernel(tc, x, w_emb, b_emb, w_ih_words, w_ih_scales, b_ih,
 
         w32 = w_ih_words.rearrange("g p n t -> g p (n t)").bitcast(I32)
         wtiles = []
-        for ci, (gate, c0, cols, by_group) in enumerate(CHUNKS):
-            wt = keep.tile([P, GROUPS, cols], I32, name="wt%d" % ci, align_bytes=64)
+        for li, (gate, g0, ng, c0, cols) in enumerate(LOADS):
+            wt = keep.tile([P, ng, cols], I32, name="w%d" % li, align_bytes=64)
             n0 = GATE_OFF[gate] + c0
-            if by_group:
-                for g in range(GROUPS):
-                    nc.sync.dma_start(out=wt[:, g, :], in_=w32[g, :, n0 : n0 + cols])
-            else:
-                nc.sync.dma_start(out=wt[:], in_=w32[:, :, n0 : n0 + cols].rearrange("g p n -> p g n"))
+            nc.sync.dma_start(out=wt[:], in_=w32[g0 : g0 + ng, :, n0 : n0 + cols].rearrange("g p n -> p g n"))
             wtiles.append(wt)
 
         ident_bf = keep.tile([P, P], BF16, name="ident_bf")
@@ -99,17 +101,19 @@ def tile_encoderrnn_w_kernel(tc, x, w_emb, b_emb, w_ih_words, w_ih_scales, b_ih,
         for d0, d1, ds, s0, s1, ss in PERM_COPIES:
             nc.vector.tensor_copy(out=perm[:, d0:d1:ds], in_=ident_bf[:, s0:s1:ss])
 
-        xb_ps = psum.tile([P, 2, P], BF16, name="xb_ps", tag="tr", bufs=2)
+        xb_ps = psum.tile([P, 2, P], BF16, name="xb_ps", tag="bank")
         nc.tensor.transpose(xb_ps[:, 0, :], x_sb[:], perm[:])
         nc.tensor.transpose(xb_ps[:, 1, :], brow[:], ident_bf[:])
         xT = keep.tile([P, P], BF16, name="xT")
         nc.vector.tensor_copy(out=xT[:], in_=xb_ps[:, 0, :])
         bT = keep.tile([P, P], F32, name="bT")
         nc.vector.tensor_copy(out=bT[:], in_=xb_ps[:, 1, :])
+        bTb = keep.tile([P, P], BF16, name="bTb")
+        nc.vector.tensor_copy(out=bTb[:], in_=xb_ps[:, 1, :])
 
         wT = keep.tile([P, 16, P], BF16, name="wT")
         for h in range(2):
-            wT_ps = psum.tile([P, 8, P], BF16, name="wT_ps", tag="acc", bufs=6)
+            wT_ps = psum.tile([P, 8, P], BF16, name="wT_ps", tag="bank")
             for q in range(8):
                 nc.tensor.transpose(wT_ps[:, q, :], w_sb[:, 8 * h + q, :], ident_bf[:])
             if h == 0:
@@ -117,14 +121,9 @@ def tile_encoderrnn_w_kernel(tc, x, w_emb, b_emb, w_ih_words, w_ih_scales, b_ih,
             else:
                 nc.scalar.copy(out=wT[:, 8:16, :], in_=wT_ps[:])
 
-        brz = keep.tile([P, 32], F32, name="brz")
-        nc.vector.tensor_tensor(out=brz[:], in0=bT[:, 0:32], in1=bT[:, 48:80], op=ALU.add)
-        bzn = keep.tile([P, 16], F32, name="bzn")
-        nc.vector.tensor_scalar(out=bzn[:], in0=brz[:, 16:32], scalar1=-1.0, scalar2=None, op0=ALU.mult)
-
         grouped = keep.tile([P, GROUPS, P, 4], BF16, name="grouped", align_bytes=64)
         for g in range(GROUPS):
-            e_ps = psum.tile([P, 4, P], F32, name="e_ps", tag="acc", bufs=6)
+            e_ps = psum.tile([P, 4, P], F32, name="e_ps", tag="bank")
             for t in range(4):
                 nc.tensor.matmul(e_ps[:, t, :], lhsT=wT[:, 4 * g + t, :], rhs=xT[:], start=True, stop=True)
             nc.vector.tensor_tensor(
@@ -141,73 +140,94 @@ def tile_encoderrnn_w_kernel(tc, x, w_emb, b_emb, w_ih_words, w_ih_scales, b_ih,
             in_=grouped[:].rearrange("p g k t -> p (g k t)"),
         )
 
-        def passes(wt, lc, n0):
-            acc = psum.tile([P, P], F32, name="acc", tag="acc", bufs=6)
-            for g in range(GROUPS):
-                nc.tensor.matmul_mx(
-                    out=acc[:],
-                    lhsT=wt[:, g, lc : lc + P].bitcast(FP8X4),
-                    lhsT_scale=planes[4 * g : P, n0 : n0 + P],
-                    rhs=ecodes[:, g * P : (g + 1) * P].bitcast(FP8X4),
-                    rhs_scale=eplane[:, g * P : (g + 1) * P],
-                    start=(g == 0),
-                    stop=(g == GROUPS - 1),
-                )
-            return acc
+        brz = keep.tile([P, 32], F32, name="brz")
+        nc.vector.tensor_tensor(out=brz[:], in0=bT[:, 0:32], in1=bT[:, 48:80], op=ALU.add)
+
+        def spread_f32(dst, first):
+            for c in range(NB):
+                bc = psum.tile([P, 4, P], F32, name="bc", tag="bank")
+                for q in range(4):
+                    col = first + 4 * c + q
+                    nc.tensor.transpose(bc[:, q, :], brz[:, col : col + 1].to_broadcast([P, P]), ident_f[:])
+                nc.scalar.copy(out=dst[:, c * BANK : (c + 1) * BANK], in_=bc[:].rearrange("p q k -> p (q k)"))
+
+        def spread_bf16(dst, first):
+            for c in range(2):
+                bc = psum.tile([P, 8, P], BF16, name="bcb", tag="bank")
+                for q in range(8):
+                    col = first + 8 * c + q
+                    nc.tensor.transpose(bc[:, q, :], bTb[:, col : col + 1].to_broadcast([P, P]), ident_bf[:])
+                nc.scalar.copy(out=dst[:, c * 1024 : (c + 1) * 1024], in_=bc[:].rearrange("p q k -> p (q k)"))
+
+        b_r = keep.tile([P, HID], F32, name="b_r")
+        b_z = keep.tile([P, HID], F32, name="b_z")
+        b_in = keep.tile([P, HID], BF16, name="b_in")
+        b_hn = keep.tile([P, HID], BF16, name="b_hn")
+        spread_f32(b_r, 0)
+        spread_bf16(b_hn, 80)
+        spread_bf16(b_in, 32)
+        spread_f32(b_z, 16)
+
+        def one_pass(acc, wt, gl, lc, gate, g, c):
+            n0 = GATE_OFF[gate] + c * BANK
+            nc.tensor.matmul_mx(
+                out=acc[:],
+                lhsT=ecodes[:, g * P : (g + 1) * P].bitcast(FP8X4),
+                lhsT_scale=eplane[:, g * P : (g + 1) * P],
+                rhs=wt[:, gl, lc : lc + BANK].bitcast(FP8X4),
+                rhs_scale=planes[4 * g : P, n0 : n0 + BANK],
+                start=(g == 0),
+                stop=(g == GROUPS - 1),
+            )
 
         out_h = out_0.rearrange("b s j -> (b s) j")
         out_l = out_1.rearrange("o b j -> (o b) j")
-        r_t = {}
+        o_tiles = {}
+        for gi, (s0, sw) in enumerate(STORE_GROUPS):
+            o_tiles[gi] = keep.tile([P, sw], F32, name="o_sb%d" % gi)
+        rb = {}
         n_t = {}
 
-        o_tiles = {}
-        for gi, (g0, gw) in enumerate(STORE_GROUPS):
-            o_tiles[gi] = keep.tile([P, gw], F32, name="o_sb%d" % gi)
-
-        def finish(c0, hts):
-            width = P * len(hts)
-            tr = psum.tile([P, width], F32, name="tr", tag="tr", bufs=2)
-            for q, ht in enumerate(hts):
-                nc.tensor.transpose(tr[:, q * P : (q + 1) * P], ht[:], ident_f[:])
-            for gi, (g0, gw) in enumerate(STORE_GROUPS):
-                if g0 <= c0 < g0 + gw:
-                    o_sb = o_tiles[gi]
-                    nc.vector.tensor_copy(out=o_sb[:, c0 - g0 : c0 - g0 + width], in_=tr[:])
-                    if c0 + width == g0 + gw:
-                        for p0, p1, ps, r0, rows in STORE_SETS:
-                            nc.sync.dma_start(out=out_h[r0 : r0 + rows, g0 : g0 + gw], in_=o_sb[p0:p1:ps, :])
-                        nc.sync.dma_start(out=out_l[:, g0 : g0 + gw], in_=o_sb[115:128:4, :])
-
-        pending = []
-        for ci, (gate, c0, cols, by_group) in enumerate(CHUNKS):
-            wt = wtiles[ci]
-            for s0 in range(0, cols, 512):
-                sub = min(512, cols - s0)
-                hts = []
-                for lc in range(s0, s0 + sub, P):
-                    j = (c0 + lc) // P
-                    acc = passes(wt, lc, GATE_OFF[gate] + c0 + lc)
-                    if gate == "r":
-                        r_j = keep.tile([P, P], F32, name="r%d" % j)
-                        nc.scalar.activation(out=r_j[:], in_=acc[:], func=ACT.Sigmoid, bias=brz[:, j : j + 1], scale=1.0)
-                        r_t[j] = r_j
-                    elif gate == "n":
-                        u = work.tile([P, P], F32, name="u")
-                        nc.vector.scalar_tensor_tensor(
-                            out=u[:], in0=r_t[j][:], scalar=bT[:, 80 + j : 81 + j], in1=acc[:], op0=ALU.mult, op1=ALU.add
-                        )
-                        n_j = keep.tile([P, P], F32, name="n%d" % j)
-                        nc.scalar.activation(out=n_j[:], in_=u[:], func=ACT.Tanh, bias=bT[:, 32 + j : 33 + j], scale=1.0)
-                        n_t[j] = n_j
-                    else:
-                        zc = work.tile([P, P], F32, name="zc")
-                        nc.scalar.activation(out=zc[:], in_=acc[:], func=ACT.Sigmoid, bias=bzn[:, j : j + 1], scale=-1.0)
-                        ht = work.tile([P, P], F32, name="ht", bufs=8)
-                        nc.vector.tensor_tensor(out=ht[:], in0=zc[:], in1=n_t[j][:], op=ALU.mult)
-                        hts.append(ht)
-                if gate == "z":
-                    for args in pending:
-                        finish(args[0], args[1])
-                    pending = [(c0 + s0, hts)]
-        for args in pending:
-            finish(args[0], args[1])
+        accs = {}
+        for li, (gate, g0, ng, c0, cols) in enumerate(LOADS):
+            banks = range(c0 // BANK, (c0 + cols) // BANK)
+            for c in banks:
+                if g0 == 0:
+                    accs[(gate, c)] = psum.tile([P, BANK], F32, name="acc_%s%d" % (gate, c), tag="bank")
+                for gl in range(ng):
+                    one_pass(accs[(gate, c)], wtiles[li], gl, c * BANK - c0, gate, g0 + gl, c)
+            if g0 + ng < GROUPS:
+                continue
+            for c in banks:
+                acc = accs[(gate, c)]
+                cs = slice(c * BANK, (c + 1) * BANK)
+                if gate == "r":
+                    a = work.tile([P, BANK], F32, name="a")
+                    nc.vector.tensor_tensor(out=a[:], in0=acc[:], in1=b_r[:, cs], op=ALU.add)
+                    r = work.tile([P, BANK], F32, name="r")
+                    nc.scalar.activation(out=r[:], in_=a[:], func=ACT.Sigmoid)
+                    c1 = work.tile([P, BANK], F32, name="c1")
+                    nc.vector.tensor_tensor(out=c1[:], in0=r[:], in1=b_hn[:, cs], op=ALU.mult)
+                    c2 = keep.tile([P, BANK], F32, name="c2_%d" % c)
+                    nc.vector.tensor_tensor(out=c2[:], in0=c1[:], in1=b_in[:, cs], op=ALU.add)
+                    rb[c] = c2
+                elif gate == "n":
+                    u = work.tile([P, BANK], F32, name="u")
+                    nc.vector.tensor_tensor(out=u[:], in0=acc[:], in1=rb[c][:], op=ALU.add)
+                    n_c = keep.tile([P, BANK], F32, name="n_%d" % c)
+                    nc.scalar.activation(out=n_c[:], in_=u[:], func=ACT.Tanh)
+                    n_t[c] = n_c
+                else:
+                    a = work.tile([P, BANK], F32, name="a")
+                    nc.vector.tensor_tensor(out=a[:], in0=acc[:], in1=b_z[:, cs], op=ALU.add)
+                    zc = work.tile([P, BANK], F32, name="zc")
+                    nc.scalar.activation(out=zc[:], in_=a[:], func=ACT.Sigmoid, scale=-1.0)
+                    for gi, (s0, sw) in enumerate(STORE_GROUPS):
+                        if s0 <= c * BANK < s0 + sw:
+                            o_sb = o_tiles[gi]
+                            lo = c * BANK - s0
+                            nc.vector.tensor_tensor(out=o_sb[:, lo : lo + BANK], in0=zc[:], in1=n_t[c][:], op=ALU.mult)
+                            if (c + 1) * BANK == s0 + sw:
+                                for p0, p1, ps, r0, rows in STORE_SETS:
+                                    nc.sync.dma_start(out=out_h[r0 : r0 + rows, s0 : s0 + sw], in_=o_sb[p0:p1:ps, :])
+                                nc.sync.dma_start(out=out_l[:, s0 : s0 + sw], in_=o_sb[115:128:4, :])

@@ -51,7 +51,7 @@ def tile_encoderrnn_w_kernel(tc, x, w_emb, b_emb, w_ih_words, w_ih_scales, b_ih,
     nc = tc.nc
     with ExitStack() as ctx:
         keep = ctx.enter_context(tc.tile_pool(name="keep", bufs=1))
-        work = ctx.enter_context(tc.tile_pool(name="work", bufs=3))
+        work = ctx.enter_context(tc.tile_pool(name="work", bufs=4))
         psum = ctx.enter_context(tc.psum_pool(name="psum", bufs=8))
 
         planes = keep.tile([P, 3 * HID], U8, name="planes", align_bytes=64)
@@ -163,10 +163,6 @@ def tile_encoderrnn_w_kernel(tc, x, w_emb, b_emb, w_ih_words, w_ih_scales, b_ih,
         b_z = keep.tile([P, HID], F32, name="b_z")
         b_in = keep.tile([P, HID], BF16, name="b_in")
         b_hn = keep.tile([P, HID], BF16, name="b_hn")
-        spread_f32(b_r, 0)
-        spread_bf16(b_hn, 80)
-        spread_bf16(b_in, 32)
-        spread_f32(b_z, 16)
 
         def one_pass(acc, wt, gl, lc, gate, g, c):
             n0 = GATE_OFF[gate] + c * BANK
@@ -187,47 +183,72 @@ def tile_encoderrnn_w_kernel(tc, x, w_emb, b_emb, w_ih_words, w_ih_scales, b_ih,
             o_tiles[gi] = keep.tile([P, sw], F32, name="o_sb%d" % gi)
         rb = {}
         n_t = {}
-
         accs = {}
-        for li, (gate, g0, ng, c0, cols) in enumerate(LOADS):
-            banks = range(c0 // BANK, (c0 + cols) // BANK)
-            for c in banks:
+
+        def passes(li):
+            gate, g0, ng, c0, cols = LOADS[li]
+            for c in range(c0 // BANK, (c0 + cols) // BANK):
                 if g0 == 0:
                     accs[(gate, c)] = psum.tile([P, BANK], F32, name="acc_%s%d" % (gate, c), tag="bank")
                 for gl in range(ng):
                     one_pass(accs[(gate, c)], wtiles[li], gl, c * BANK - c0, gate, g0 + gl, c)
+
+        def cols_of(c):
+            return slice(c * BANK, (c + 1) * BANK)
+
+        spread_f32(b_r, 0)
+        for li in range(0, 4):
+            passes(li)
+        spread_bf16(b_hn, 80)
+        spread_bf16(b_in, 32)
+        a_r = {}
+        for c in range(NB):
+            a_r[c] = work.tile([P, BANK], F32, name="a")
+            nc.vector.tensor_tensor(out=a_r[c][:], in0=accs[("r", c)][:], in1=b_r[:, cols_of(c)], op=ALU.add)
+        r_t = {}
+        for c in range(NB):
+            r_t[c] = work.tile([P, BANK], F32, name="r")
+            nc.scalar.activation(out=r_t[c][:], in_=a_r[c][:], func=ACT.Sigmoid)
+        for c in range(NB):
+            c1 = work.tile([P, BANK], F32, name="c1")
+            nc.vector.tensor_tensor(out=c1[:], in0=r_t[c][:], in1=b_hn[:, cols_of(c)], op=ALU.mult)
+            c2 = keep.tile([P, BANK], F32, name="c2_%d" % c)
+            nc.vector.tensor_tensor(out=c2[:], in0=c1[:], in1=b_in[:, cols_of(c)], op=ALU.add)
+            rb[c] = c2
+
+        for li in range(4, 8):
+            passes(li)
+        spread_f32(b_z, 16)
+        u_t = {}
+        for c in range(NB):
+            u_t[c] = work.tile([P, BANK], F32, name="u")
+            nc.vector.tensor_tensor(out=u_t[c][:], in0=accs[("n", c)][:], in1=rb[c][:], op=ALU.add)
+        for c in range(NB):
+            n_c = keep.tile([P, BANK], F32, name="n_%d" % c)
+            nc.scalar.activation(out=n_c[:], in_=u_t[c][:], func=ACT.Tanh)
+            n_t[c] = n_c
+
+        for li in range(8, len(LOADS)):
+            gate, g0, ng, c0, cols = LOADS[li]
+            passes(li)
             if g0 + ng < GROUPS:
                 continue
+            banks = range(c0 // BANK, (c0 + cols) // BANK)
+            a_z = {}
+            z_t = {}
             for c in banks:
-                acc = accs[(gate, c)]
-                cs = slice(c * BANK, (c + 1) * BANK)
-                if gate == "r":
-                    a = work.tile([P, BANK], F32, name="a")
-                    nc.vector.tensor_tensor(out=a[:], in0=acc[:], in1=b_r[:, cs], op=ALU.add)
-                    r = work.tile([P, BANK], F32, name="r")
-                    nc.scalar.activation(out=r[:], in_=a[:], func=ACT.Sigmoid)
-                    c1 = work.tile([P, BANK], F32, name="c1")
-                    nc.vector.tensor_tensor(out=c1[:], in0=r[:], in1=b_hn[:, cs], op=ALU.mult)
-                    c2 = keep.tile([P, BANK], F32, name="c2_%d" % c)
-                    nc.vector.tensor_tensor(out=c2[:], in0=c1[:], in1=b_in[:, cs], op=ALU.add)
-                    rb[c] = c2
-                elif gate == "n":
-                    u = work.tile([P, BANK], F32, name="u")
-                    nc.vector.tensor_tensor(out=u[:], in0=acc[:], in1=rb[c][:], op=ALU.add)
-                    n_c = keep.tile([P, BANK], F32, name="n_%d" % c)
-                    nc.scalar.activation(out=n_c[:], in_=u[:], func=ACT.Tanh)
-                    n_t[c] = n_c
-                else:
-                    a = work.tile([P, BANK], F32, name="a")
-                    nc.vector.tensor_tensor(out=a[:], in0=acc[:], in1=b_z[:, cs], op=ALU.add)
-                    zc = work.tile([P, BANK], F32, name="zc")
-                    nc.scalar.activation(out=zc[:], in_=a[:], func=ACT.Sigmoid, scale=-1.0)
-                    for gi, (s0, sw) in enumerate(STORE_GROUPS):
-                        if s0 <= c * BANK < s0 + sw:
-                            o_sb = o_tiles[gi]
-                            lo = c * BANK - s0
-                            nc.vector.tensor_tensor(out=o_sb[:, lo : lo + BANK], in0=zc[:], in1=n_t[c][:], op=ALU.mult)
-                            if (c + 1) * BANK == s0 + sw:
-                                for p0, p1, ps, r0, rows in STORE_SETS:
-                                    nc.sync.dma_start(out=out_h[r0 : r0 + rows, s0 : s0 + sw], in_=o_sb[p0:p1:ps, :])
-                                nc.sync.dma_start(out=out_l[:, s0 : s0 + sw], in_=o_sb[115:128:4, :])
+                a_z[c] = work.tile([P, BANK], F32, name="a")
+                nc.vector.tensor_tensor(out=a_z[c][:], in0=accs[("z", c)][:], in1=b_z[:, cols_of(c)], op=ALU.add)
+            for c in banks:
+                z_t[c] = work.tile([P, BANK], F32, name="zc")
+                nc.scalar.activation(out=z_t[c][:], in_=a_z[c][:], func=ACT.Sigmoid, scale=-1.0)
+            for c in banks:
+                for gi, (s0, sw) in enumerate(STORE_GROUPS):
+                    if s0 <= c * BANK < s0 + sw:
+                        o_sb = o_tiles[gi]
+                        lo = c * BANK - s0
+                        nc.vector.tensor_tensor(out=o_sb[:, lo : lo + BANK], in0=z_t[c][:], in1=n_t[c][:], op=ALU.mult)
+                        if (c + 1) * BANK == s0 + sw:
+                            for p0, p1, ps, r0, rows in STORE_SETS:
+                                nc.sync.dma_start(out=out_h[r0 : r0 + rows, s0 : s0 + sw], in_=o_sb[p0:p1:ps, :])
+                            nc.sync.dma_start(out=out_l[:, s0 : s0 + sw], in_=o_sb[115:128:4, :])

@@ -29,11 +29,19 @@ LOADS = [
     ("n", 1, 1, 0, 2048),
     ("n", 2, 1, 0, 2048),
     ("n", 3, 1, 0, 2048),
-    ("z", 0, 4, 0, 1024),
+    ("z", 0, 2, 0, 1024),
+    ("z", 2, 2, 0, 1024),
     ("z", 0, 4, 1024, 512),
     ("z", 0, 3, 1536, 512),
     ("z", 3, 1, 1536, 512),
 ]
+GATE_LOADS = {"r": [0, 1, 2, 3], "n": [4, 5, 6, 7], "z": [8, 9, 10, 11, 12]}
+UNITS = {
+    "r": [(0, 512), (512, 512), (1024, 512), (1536, 512)],
+    "n": [(0, 512), (512, 512), (1024, 512), (1536, 512)],
+    "z": [(0, 512), (512, 512), (1024, 512), (1536, 512)],
+}
+POOL_MULT_BELOW = 0
 STORE_GROUPS = [(0, 1024), (1024, 512), (1536, 512)]
 STORE_SETS = [(0, 128, 2, 0, 64), (1, 128, 4, 64, 32), (3, 67, 4, 96, 16), (67, 99, 4, 112, 8), (99, 115, 4, 120, 4)]
 PERM_COPIES = [
@@ -54,13 +62,15 @@ def tile_encoderrnn_w_kernel(tc, x, w_emb, b_emb, w_ih_words, w_ih_scales, b_ih,
         work = ctx.enter_context(tc.tile_pool(name="work", bufs=4))
         psum = ctx.enter_context(tc.psum_pool(name="psum", bufs=8))
 
-        planes = keep.tile([P, 3 * HID], U8, name="planes", align_bytes=64)
-        nc.vector.memset(planes[:].bitcast(I32), 0)
-        warm = keep.tile([P, 1], F32, name="warm")
-        nc.vector.memset(warm[:], 0.0)
-        warm2 = keep.tile([P, 1], F32, name="warm2")
-        nc.scalar.activation(out=warm2[:], in_=warm[:], func=ACT.Sigmoid)
-
+        be_sb = keep.tile([P, 16], BF16, name="be_sb")
+        nc.scalar.dma_start(
+            out=be_sb[:].rearrange("p (g t) -> p g t", t=4),
+            in_=b_emb.rearrange("(g p t) -> p g t", g=GROUPS, p=P, t=4),
+        )
+        brow = keep.tile([P, P], BF16, name="brow")
+        nc.vector.memset(brow[96:128, :], 0.0)
+        nc.scalar.dma_start(out=brow[0:48, :], in_=b_ih.rearrange("(r c) -> r c", c=P))
+        nc.scalar.dma_start(out=brow[48:96, :], in_=b_hh.rearrange("(r c) -> r c", c=P))
         x_sb = keep.tile([P, P], BF16, name="x_sb")
         nc.sync.dma_start(out=x_sb[:], in_=x.rearrange("b s i -> (b s) i"))
         w_sb = keep.tile([P, 16, P], BF16, name="w_sb")
@@ -68,15 +78,12 @@ def tile_encoderrnn_w_kernel(tc, x, w_emb, b_emb, w_ih_words, w_ih_scales, b_ih,
             out=w_sb[:].rearrange("p (g t) i -> p g (t i)", t=4),
             in_=w_emb.rearrange("(g p t) i -> p g (t i)", g=GROUPS, p=P, t=4),
         )
-        be_sb = keep.tile([P, 16], BF16, name="be_sb")
-        nc.scalar.dma_start(
-            out=be_sb[:].rearrange("p (g t) -> p g t", t=4),
-            in_=b_emb.rearrange("(g p t) -> p g t", g=GROUPS, p=P, t=4),
-        )
-        brow = keep.tile([P, P], BF16, name="brow")
-        nc.vector.memset(brow[:], 0.0)
-        nc.scalar.dma_start(out=brow[0:48, :], in_=b_ih.rearrange("(r c) -> r c", c=P))
-        nc.scalar.dma_start(out=brow[48:96, :], in_=b_hh.rearrange("(r c) -> r c", c=P))
+        warm = keep.tile([P, 1], F32, name="warm")
+        nc.vector.memset(warm[:], 0.0)
+        warm2 = keep.tile([P, 1], F32, name="warm2")
+        nc.scalar.activation(out=warm2[:], in_=warm[:], func=ACT.Sigmoid)
+        planes = keep.tile([P, 3 * HID], U8, name="planes", align_bytes=64)
+        nc.vector.memset(planes[:].bitcast(I32), 0)
 
         sc32 = w_ih_scales.bitcast(I32)
         for q in range(4):
@@ -101,15 +108,10 @@ def tile_encoderrnn_w_kernel(tc, x, w_emb, b_emb, w_ih_words, w_ih_scales, b_ih,
         for d0, d1, ds, s0, s1, ss in PERM_COPIES:
             nc.vector.tensor_copy(out=perm[:, d0:d1:ds], in_=ident_bf[:, s0:s1:ss])
 
-        xb_ps = psum.tile([P, 2, P], BF16, name="xb_ps", tag="bank")
-        nc.tensor.transpose(xb_ps[:, 0, :], x_sb[:], perm[:])
-        nc.tensor.transpose(xb_ps[:, 1, :], brow[:], ident_bf[:])
+        x_ps = psum.tile([P, P], BF16, name="x_ps", tag="bank")
+        nc.tensor.transpose(x_ps[:], x_sb[:], perm[:])
         xT = keep.tile([P, P], BF16, name="xT")
-        nc.vector.tensor_copy(out=xT[:], in_=xb_ps[:, 0, :])
-        bT = keep.tile([P, P], F32, name="bT")
-        nc.vector.tensor_copy(out=bT[:], in_=xb_ps[:, 1, :])
-        bTb = keep.tile([P, P], BF16, name="bTb")
-        nc.vector.tensor_copy(out=bTb[:], in_=xb_ps[:, 1, :])
+        nc.vector.tensor_copy(out=xT[:], in_=x_ps[:])
 
         wT = keep.tile([P, 16, P], BF16, name="wT")
         for h in range(2):
@@ -140,6 +142,12 @@ def tile_encoderrnn_w_kernel(tc, x, w_emb, b_emb, w_ih_words, w_ih_scales, b_ih,
             in_=grouped[:].rearrange("p g k t -> p (g k t)"),
         )
 
+        b_ps = psum.tile([P, P], BF16, name="b_ps", tag="bank")
+        nc.tensor.transpose(b_ps[:], brow[:], ident_bf[:])
+        bT = keep.tile([P, P], F32, name="bT")
+        nc.vector.tensor_copy(out=bT[:], in_=b_ps[:])
+        bTb = keep.tile([P, P], BF16, name="bTb")
+        nc.vector.tensor_copy(out=bTb[:], in_=b_ps[:])
         brz = keep.tile([P, 32], F32, name="brz")
         nc.vector.tensor_tensor(out=brz[:], in0=bT[:, 0:32], in1=bT[:, 48:80], op=ALU.add)
 
@@ -164,91 +172,84 @@ def tile_encoderrnn_w_kernel(tc, x, w_emb, b_emb, w_ih_words, w_ih_scales, b_ih,
         b_in = keep.tile([P, HID], BF16, name="b_in")
         b_hn = keep.tile([P, HID], BF16, name="b_hn")
 
-        def one_pass(acc, wt, gl, lc, gate, g, c):
-            n0 = GATE_OFF[gate] + c * BANK
-            nc.tensor.matmul_mx(
-                out=acc[:],
-                lhsT=ecodes[:, g * P : (g + 1) * P].bitcast(FP8X4),
-                lhsT_scale=eplane[:, g * P : (g + 1) * P],
-                rhs=wt[:, gl, lc : lc + BANK].bitcast(FP8X4),
-                rhs_scale=planes[4 * g : P, n0 : n0 + BANK],
-                start=(g == 0),
-                stop=(g == GROUPS - 1),
-            )
-
         out_h = out_0.rearrange("b s j -> (b s) j")
         out_l = out_1.rearrange("o b j -> (o b) j")
-        o_tiles = {}
-        for gi, (s0, sw) in enumerate(STORE_GROUPS):
-            o_tiles[gi] = keep.tile([P, sw], F32, name="o_sb%d" % gi)
-        rb = {}
-        n_t = {}
         accs = {}
 
         def passes(li):
             gate, g0, ng, c0, cols = LOADS[li]
-            for c in range(c0 // BANK, (c0 + cols) // BANK):
+            for u0, uw in UNITS[gate]:
+                if u0 < c0 or u0 >= c0 + cols:
+                    continue
                 if g0 == 0:
-                    accs[(gate, c)] = psum.tile([P, BANK], F32, name="acc_%s%d" % (gate, c), tag="bank")
+                    accs[(gate, u0)] = psum.tile([P, uw], F32, name="acc_%s%d" % (gate, u0), tag="bank")
                 for gl in range(ng):
-                    one_pass(accs[(gate, c)], wtiles[li], gl, c * BANK - c0, gate, g0 + gl, c)
-
-        def cols_of(c):
-            return slice(c * BANK, (c + 1) * BANK)
+                    g = g0 + gl
+                    n0 = GATE_OFF[gate] + u0
+                    nc.tensor.matmul_mx(
+                        out=accs[(gate, u0)][:],
+                        lhsT=ecodes[:, g * P : (g + 1) * P].bitcast(FP8X4),
+                        lhsT_scale=eplane[:, g * P : (g + 1) * P],
+                        rhs=wtiles[li][:, gl, u0 - c0 : u0 - c0 + uw].bitcast(FP8X4),
+                        rhs_scale=planes[4 * g : P, n0 : n0 + uw],
+                        start=(g == 0),
+                        stop=(g == GROUPS - 1),
+                    )
 
         spread_f32(b_r, 0)
-        for li in range(0, 4):
+        for li in GATE_LOADS["r"]:
             passes(li)
         spread_bf16(b_hn, 80)
         spread_bf16(b_in, 32)
+        c2 = keep.tile([P, HID], F32, name="c2")
         a_r = {}
-        for c in range(NB):
-            a_r[c] = work.tile([P, BANK], F32, name="a")
-            nc.vector.tensor_tensor(out=a_r[c][:], in0=accs[("r", c)][:], in1=b_r[:, cols_of(c)], op=ALU.add)
+        for u0, uw in UNITS["r"]:
+            a_r[u0] = work.tile([P, uw], F32, name="a")
+            nc.vector.tensor_tensor(out=a_r[u0][:], in0=accs[("r", u0)][:], in1=b_r[:, u0 : u0 + uw], op=ALU.add)
         r_t = {}
-        for c in range(NB):
-            r_t[c] = work.tile([P, BANK], F32, name="r")
-            nc.scalar.activation(out=r_t[c][:], in_=a_r[c][:], func=ACT.Sigmoid)
-        for c in range(NB):
-            c1 = work.tile([P, BANK], F32, name="c1")
-            nc.vector.tensor_tensor(out=c1[:], in0=r_t[c][:], in1=b_hn[:, cols_of(c)], op=ALU.mult)
-            c2 = keep.tile([P, BANK], F32, name="c2_%d" % c)
-            nc.vector.tensor_tensor(out=c2[:], in0=c1[:], in1=b_in[:, cols_of(c)], op=ALU.add)
-            rb[c] = c2
+        for u0, uw in UNITS["r"]:
+            r_t[u0] = work.tile([P, uw], F32, name="r")
+            nc.scalar.activation(out=r_t[u0][:], in_=a_r[u0][:], func=ACT.Sigmoid)
+        for u0, uw in UNITS["r"]:
+            c1 = work.tile([P, uw], F32, name="c1")
+            nc.vector.tensor_tensor(out=c1[:], in0=r_t[u0][:], in1=b_hn[:, u0 : u0 + uw], op=ALU.mult)
+            nc.vector.tensor_tensor(out=c2[:, u0 : u0 + uw], in0=c1[:], in1=b_in[:, u0 : u0 + uw], op=ALU.add)
 
-        for li in range(4, 8):
+        for li in GATE_LOADS["n"]:
             passes(li)
         spread_f32(b_z, 16)
+        n_all = keep.tile([P, HID], F32, name="n_all")
         u_t = {}
-        for c in range(NB):
-            u_t[c] = work.tile([P, BANK], F32, name="u")
-            nc.vector.tensor_tensor(out=u_t[c][:], in0=accs[("n", c)][:], in1=rb[c][:], op=ALU.add)
-        for c in range(NB):
-            n_c = keep.tile([P, BANK], F32, name="n_%d" % c)
-            nc.scalar.activation(out=n_c[:], in_=u_t[c][:], func=ACT.Tanh)
-            n_t[c] = n_c
+        for u0, uw in UNITS["n"]:
+            u_t[u0] = work.tile([P, uw], F32, name="u")
+            nc.vector.tensor_tensor(out=u_t[u0][:], in0=accs[("n", u0)][:], in1=c2[:, u0 : u0 + uw], op=ALU.add)
+        for u0, uw in UNITS["n"]:
+            nc.scalar.activation(out=n_all[:, u0 : u0 + uw], in_=u_t[u0][:], func=ACT.Tanh)
 
-        for li in range(8, len(LOADS)):
+        o_tiles = {}
+        for s0, sw in STORE_GROUPS:
+            o_tiles[s0] = keep.tile([P, sw], F32, name="o_sb%d" % s0)
+        for li in GATE_LOADS["z"]:
             gate, g0, ng, c0, cols = LOADS[li]
             passes(li)
             if g0 + ng < GROUPS:
                 continue
-            banks = range(c0 // BANK, (c0 + cols) // BANK)
+            units = [(u0, uw) for u0, uw in UNITS["z"] if c0 <= u0 < c0 + cols]
             a_z = {}
             z_t = {}
-            for c in banks:
-                a_z[c] = work.tile([P, BANK], F32, name="a")
-                nc.vector.tensor_tensor(out=a_z[c][:], in0=accs[("z", c)][:], in1=b_z[:, cols_of(c)], op=ALU.add)
-            for c in banks:
-                z_t[c] = work.tile([P, BANK], F32, name="zc")
-                nc.scalar.activation(out=z_t[c][:], in_=a_z[c][:], func=ACT.Sigmoid, scale=-1.0)
-            for c in banks:
-                for gi, (s0, sw) in enumerate(STORE_GROUPS):
-                    if s0 <= c * BANK < s0 + sw:
-                        o_sb = o_tiles[gi]
-                        lo = c * BANK - s0
-                        nc.vector.tensor_tensor(out=o_sb[:, lo : lo + BANK], in0=z_t[c][:], in1=n_t[c][:], op=ALU.mult)
-                        if (c + 1) * BANK == s0 + sw:
+            for u0, uw in units:
+                a_z[u0] = work.tile([P, uw], F32, name="a")
+                nc.vector.tensor_tensor(out=a_z[u0][:], in0=accs[("z", u0)][:], in1=b_z[:, u0 : u0 + uw], op=ALU.add)
+            for u0, uw in units:
+                z_t[u0] = work.tile([P, uw], F32, name="zc")
+                nc.scalar.activation(out=z_t[u0][:], in_=a_z[u0][:], func=ACT.Sigmoid, scale=-1.0)
+            for u0, uw in units:
+                for s0, sw in STORE_GROUPS:
+                    if s0 <= u0 < s0 + sw:
+                        o_sb = o_tiles[s0]
+                        eng = nc.gpsimd if u0 < POOL_MULT_BELOW else nc.vector
+                        eng.tensor_tensor(out=o_sb[:, u0 - s0 : u0 - s0 + uw], in0=z_t[u0][:], in1=n_all[:, u0 : u0 + uw], op=ALU.mult)
+                        if u0 + uw == s0 + sw:
                             for p0, p1, ps, r0, rows in STORE_SETS:
                                 nc.sync.dma_start(out=out_h[r0 : r0 + rows, s0 : s0 + sw], in_=o_sb[p0:p1:ps, :])
                             nc.sync.dma_start(out=out_l[:, s0 : s0 + sw], in_=o_sb[115:128:4, :])

@@ -29,21 +29,14 @@ LOADS = [
     ("n", 1, 1, 0, 2048),
     ("n", 2, 1, 0, 2048),
     ("n", 3, 1, 0, 2048),
-    ("z", 0, 2, 0, 1024),
-    ("z", 2, 2, 0, 1024),
+    ("z", 0, 4, 0, 512),
+    ("z", 0, 4, 512, 512),
     ("z", 0, 4, 1024, 512),
     ("z", 0, 3, 1536, 512),
     ("z", 3, 1, 1536, 512),
 ]
-GATE_LOADS = {"r": [0, 1, 2, 3], "n": [4, 5, 6, 7], "z": [8, 9, 10, 11, 12]}
-UNITS = {
-    "r": [(0, 512), (512, 512), (1024, 512), (1536, 512)],
-    "n": [(0, 512), (512, 512), (1024, 512), (1536, 512)],
-    "z": [(0, 512), (512, 512), (1024, 512), (1536, 512)],
-}
-POOL_MULT_BELOW = 0
-STORE_GROUPS = [(0, 1024), (1024, 512), (1536, 512)]
-STORE_SETS = [(0, 128, 2, 0, 64), (1, 128, 4, 64, 32), (3, 67, 4, 96, 16), (67, 99, 4, 112, 8), (99, 115, 4, 120, 4)]
+BIG_SETS = [(0, 128, 2, 0, 64), (1, 128, 4, 64, 32), (3, 67, 4, 96, 16)]
+SMALL_SETS = [(67, 99, 4, 112, 8), (99, 115, 4, 120, 4)]
 PERM_COPIES = [
     (0, 62, 2, 0, 31, 1),
     (62, 124, 2, 32, 63, 1),
@@ -61,6 +54,7 @@ def tile_encoderrnn_w_kernel(tc, x, w_emb, b_emb, w_ih_words, w_ih_scales, b_ih,
         keep = ctx.enter_context(tc.tile_pool(name="keep", bufs=1))
         work = ctx.enter_context(tc.tile_pool(name="work", bufs=4))
         psum = ctx.enter_context(tc.psum_pool(name="psum", bufs=8))
+        ctx.enter_context(tc.manual_schedule())
 
         be_sb = keep.tile([P, 16], BF16, name="be_sb")
         nc.scalar.dma_start(
@@ -134,6 +128,10 @@ def tile_encoderrnn_w_kernel(tc, x, w_emb, b_emb, w_ih_words, w_ih_scales, b_ih,
                 in1=be_sb[:, 4 * g : 4 * g + 4].unsqueeze(1).to_broadcast([P, P, 4]),
                 op=ALU.add,
             )
+        b_ps = psum.tile([P, P], BF16, name="b_ps", tag="bank")
+        nc.tensor.transpose(b_ps[:], brow[:], ident_bf[:])
+        bT = keep.tile([P, P], F32, name="bT")
+        nc.vector.tensor_copy(out=bT[:], in_=b_ps[:])
         ecodes = keep.tile([P, GROUPS * P], U32, name="ecodes", align_bytes=64)
         eplane = keep.tile([P, GROUPS * P], U8, name="eplane", align_bytes=64)
         nc.vector.quantize_mx(
@@ -142,14 +140,10 @@ def tile_encoderrnn_w_kernel(tc, x, w_emb, b_emb, w_ih_words, w_ih_scales, b_ih,
             in_=grouped[:].rearrange("p g k t -> p (g k t)"),
         )
 
-        b_ps = psum.tile([P, P], BF16, name="b_ps", tag="bank")
-        nc.tensor.transpose(b_ps[:], brow[:], ident_bf[:])
-        bT = keep.tile([P, P], F32, name="bT")
-        nc.vector.tensor_copy(out=bT[:], in_=b_ps[:])
-        bTb = keep.tile([P, P], BF16, name="bTb")
-        nc.vector.tensor_copy(out=bTb[:], in_=b_ps[:])
         brz = keep.tile([P, 32], F32, name="brz")
         nc.vector.tensor_tensor(out=brz[:], in0=bT[:, 0:32], in1=bT[:, 48:80], op=ALU.add)
+        bTb = keep.tile([P, P], BF16, name="bTb")
+        nc.vector.tensor_copy(out=bTb[:], in_=b_ps[:])
 
         def spread_f32(dst, first):
             for c in range(NB):
@@ -178,78 +172,90 @@ def tile_encoderrnn_w_kernel(tc, x, w_emb, b_emb, w_ih_words, w_ih_scales, b_ih,
 
         def passes(li):
             gate, g0, ng, c0, cols = LOADS[li]
-            for u0, uw in UNITS[gate]:
-                if u0 < c0 or u0 >= c0 + cols:
-                    continue
+            for c in range(c0 // BANK, (c0 + cols) // BANK):
                 if g0 == 0:
-                    accs[(gate, u0)] = psum.tile([P, uw], F32, name="acc_%s%d" % (gate, u0), tag="bank")
+                    accs[(gate, c)] = psum.tile([P, BANK], F32, name="acc_%s%d" % (gate, c), tag="bank")
                 for gl in range(ng):
                     g = g0 + gl
-                    n0 = GATE_OFF[gate] + u0
+                    n0 = GATE_OFF[gate] + c * BANK
                     nc.tensor.matmul_mx(
-                        out=accs[(gate, u0)][:],
+                        out=accs[(gate, c)][:],
                         lhsT=ecodes[:, g * P : (g + 1) * P].bitcast(FP8X4),
                         lhsT_scale=eplane[:, g * P : (g + 1) * P],
-                        rhs=wtiles[li][:, gl, u0 - c0 : u0 - c0 + uw].bitcast(FP8X4),
-                        rhs_scale=planes[4 * g : P, n0 : n0 + uw],
+                        rhs=wtiles[li][:, gl, c * BANK - c0 : (c + 1) * BANK - c0].bitcast(FP8X4),
+                        rhs_scale=planes[4 * g : P, n0 : n0 + BANK],
                         start=(g == 0),
                         stop=(g == GROUPS - 1),
                     )
 
+        def cs(c):
+            return slice(c * BANK, (c + 1) * BANK)
+
         spread_f32(b_r, 0)
-        for li in GATE_LOADS["r"]:
-            passes(li)
+        passes(0)
         spread_bf16(b_hn, 80)
+        passes(1)
         spread_bf16(b_in, 32)
-        c2 = keep.tile([P, HID], F32, name="c2")
+        passes(2)
+        passes(3)
         a_r = {}
-        for u0, uw in UNITS["r"]:
-            a_r[u0] = work.tile([P, uw], F32, name="a")
-            nc.vector.tensor_tensor(out=a_r[u0][:], in0=accs[("r", u0)][:], in1=b_r[:, u0 : u0 + uw], op=ALU.add)
         r_t = {}
-        for u0, uw in UNITS["r"]:
-            r_t[u0] = work.tile([P, uw], F32, name="r")
-            nc.scalar.activation(out=r_t[u0][:], in_=a_r[u0][:], func=ACT.Sigmoid)
-        for u0, uw in UNITS["r"]:
-            c1 = work.tile([P, uw], F32, name="c1")
-            nc.vector.tensor_tensor(out=c1[:], in0=r_t[u0][:], in1=b_hn[:, u0 : u0 + uw], op=ALU.mult)
-            nc.vector.tensor_tensor(out=c2[:, u0 : u0 + uw], in0=c1[:], in1=b_in[:, u0 : u0 + uw], op=ALU.add)
-
-        for li in GATE_LOADS["n"]:
-            passes(li)
+        for c in range(NB):
+            a_r[c] = work.tile([P, BANK], F32, name="a")
+            nc.vector.tensor_tensor(out=a_r[c][:], in0=accs[("r", c)][:], in1=b_r[:, cs(c)], op=ALU.add)
+            r_t[c] = work.tile([P, BANK], F32, name="r")
+            nc.scalar.activation(out=r_t[c][:], in_=a_r[c][:], func=ACT.Sigmoid)
+        passes(4)
         spread_f32(b_z, 16)
-        n_all = keep.tile([P, HID], F32, name="n_all")
-        u_t = {}
-        for u0, uw in UNITS["n"]:
-            u_t[u0] = work.tile([P, uw], F32, name="u")
-            nc.vector.tensor_tensor(out=u_t[u0][:], in0=accs[("n", u0)][:], in1=c2[:, u0 : u0 + uw], op=ALU.add)
-        for u0, uw in UNITS["n"]:
-            nc.scalar.activation(out=n_all[:, u0 : u0 + uw], in_=u_t[u0][:], func=ACT.Tanh)
+        c2 = keep.tile([P, HID], F32, name="c2")
+        for c0 in (0, 2):
+            c1 = {}
+            for c in (c0, c0 + 1):
+                c1[c] = work.tile([P, BANK], F32, name="c1")
+                nc.vector.tensor_tensor(out=c1[c][:], in0=r_t[c][:], in1=b_hn[:, cs(c)], op=ALU.mult)
+            for c in (c0, c0 + 1):
+                nc.vector.tensor_tensor(out=c2[:, cs(c)], in0=c1[c][:], in1=b_in[:, cs(c)], op=ALU.add)
 
-        o_tiles = {}
-        for s0, sw in STORE_GROUPS:
-            o_tiles[s0] = keep.tile([P, sw], F32, name="o_sb%d" % s0)
-        for li in GATE_LOADS["z"]:
-            gate, g0, ng, c0, cols = LOADS[li]
-            passes(li)
-            if g0 + ng < GROUPS:
-                continue
-            units = [(u0, uw) for u0, uw in UNITS["z"] if c0 <= u0 < c0 + cols]
-            a_z = {}
-            z_t = {}
-            for u0, uw in units:
-                a_z[u0] = work.tile([P, uw], F32, name="a")
-                nc.vector.tensor_tensor(out=a_z[u0][:], in0=accs[("z", u0)][:], in1=b_z[:, u0 : u0 + uw], op=ALU.add)
-            for u0, uw in units:
-                z_t[u0] = work.tile([P, uw], F32, name="zc")
-                nc.scalar.activation(out=z_t[u0][:], in_=a_z[u0][:], func=ACT.Sigmoid, scale=-1.0)
-            for u0, uw in units:
-                for s0, sw in STORE_GROUPS:
-                    if s0 <= u0 < s0 + sw:
-                        o_sb = o_tiles[s0]
-                        eng = nc.gpsimd if u0 < POOL_MULT_BELOW else nc.vector
-                        eng.tensor_tensor(out=o_sb[:, u0 - s0 : u0 - s0 + uw], in0=z_t[u0][:], in1=n_all[:, u0 : u0 + uw], op=ALU.mult)
-                        if u0 + uw == s0 + sw:
-                            for p0, p1, ps, r0, rows in STORE_SETS:
-                                nc.sync.dma_start(out=out_h[r0 : r0 + rows, s0 : s0 + sw], in_=o_sb[p0:p1:ps, :])
-                            nc.sync.dma_start(out=out_l[:, s0 : s0 + sw], in_=o_sb[115:128:4, :])
+        passes(5)
+        passes(6)
+        passes(7)
+        n_all = keep.tile([P, HID], F32, name="n_all")
+        for c in range(NB):
+            u = work.tile([P, BANK], F32, name="u")
+            nc.vector.tensor_tensor(out=u[:], in0=accs[("n", c)][:], in1=c2[:, cs(c)], op=ALU.add)
+            nc.scalar.activation(out=n_all[:, cs(c)], in_=u[:], func=ACT.Tanh)
+
+        o_all = keep.tile([P, HID], F32, name="o_all")
+        z_t = {}
+
+        def z_front(c):
+            a = work.tile([P, BANK], F32, name="a")
+            nc.vector.tensor_tensor(out=a[:], in0=accs[("z", c)][:], in1=b_z[:, cs(c)], op=ALU.add)
+            z_t[c] = work.tile([P, BANK], F32, name="zc")
+            nc.scalar.activation(out=z_t[c][:], in_=a[:], func=ACT.Sigmoid, scale=-1.0)
+
+        def z_back(eng, c):
+            eng.tensor_tensor(out=o_all[:, cs(c)], in0=z_t[c][:], in1=n_all[:, cs(c)], op=ALU.mult)
+
+        def store(eng, sets, s0, s1):
+            for p0, p1, ps, r0, rows in sets:
+                eng.dma_start(out=out_h[r0 : r0 + rows, s0:s1], in_=o_all[p0:p1:ps, s0:s1])
+
+        passes(8)
+        z_front(0)
+        z_back(nc.gpsimd, 0)
+        passes(9)
+        z_front(1)
+        z_back(nc.gpsimd, 1)
+        store(nc.sync, BIG_SETS + SMALL_SETS, 0, 1024)
+        nc.sync.dma_start(out=out_l[:, 0:1024], in_=o_all[115:128:4, 0:1024])
+        passes(10)
+        z_front(2)
+        passes(11)
+        passes(12)
+        z_front(3)
+        z_back(nc.vector, 2)
+        z_back(nc.vector, 3)
+        store(nc.sync, BIG_SETS, 1024, 2048)
+        store(nc.scalar, SMALL_SETS, 1024, 2048)
+        nc.scalar.dma_start(out=out_l[:, 1024:2048], in_=o_all[115:128:4, 1024:2048])

@@ -21,16 +21,16 @@ FLOPS = 2 * 128 * 128 * 2048 + 2 * 128 * 2048 * 6144
 
 GATE_OFF = {"r": 0, "z": HID, "n": 2 * HID}
 LOADS = [
-    ("r", 0, 1, 0, 2048),
-    ("r", 1, 1, 0, 2048),
-    ("r", 2, 1, 0, 2048),
-    ("r", 3, 1, 0, 2048),
+    ("r", 0, 2, 0, 1024),
+    ("r", 2, 2, 0, 1024),
+    ("r", 0, 2, 1024, 1024),
+    ("r", 2, 2, 1024, 1024),
     ("n", 0, 1, 0, 2048),
     ("n", 1, 1, 0, 2048),
     ("n", 2, 1, 0, 2048),
     ("n", 3, 1, 0, 2048),
-    ("z", 0, 4, 0, 512),
-    ("z", 0, 4, 512, 512),
+    ("z", 0, 2, 0, 1024),
+    ("z", 2, 2, 0, 1024),
     ("z", 0, 4, 1024, 512),
     ("z", 0, 3, 1536, 512),
     ("z", 3, 1, 1536, 512),
@@ -102,51 +102,17 @@ def tile_encoderrnn_w_kernel(tc, x, w_emb, b_emb, w_ih_words, w_ih_scales, b_ih,
         for d0, d1, ds, s0, s1, ss in PERM_COPIES:
             nc.vector.tensor_copy(out=perm[:, d0:d1:ds], in_=ident_bf[:, s0:s1:ss])
 
-        x_ps = psum.tile([P, P], BF16, name="x_ps", tag="bank")
-        nc.tensor.transpose(x_ps[:], x_sb[:], perm[:])
-        xT = keep.tile([P, P], BF16, name="xT")
-        nc.vector.tensor_copy(out=xT[:], in_=x_ps[:])
-
-        wT = keep.tile([P, 16, P], BF16, name="wT")
-        for h in range(2):
-            wT_ps = psum.tile([P, 8, P], BF16, name="wT_ps", tag="bank")
-            for q in range(8):
-                nc.tensor.transpose(wT_ps[:, q, :], w_sb[:, 8 * h + q, :], ident_bf[:])
-            if h == 0:
-                nc.vector.tensor_copy(out=wT[:, 0:8, :], in_=wT_ps[:])
-            else:
-                nc.scalar.copy(out=wT[:, 8:16, :], in_=wT_ps[:])
-
-        grouped = keep.tile([P, GROUPS, P, 4], BF16, name="grouped", align_bytes=64)
-        for g in range(GROUPS):
-            e_ps = psum.tile([P, 4, P], F32, name="e_ps", tag="bank")
-            for t in range(4):
-                nc.tensor.matmul(e_ps[:, t, :], lhsT=wT[:, 4 * g + t, :], rhs=xT[:], start=True, stop=True)
-            nc.vector.tensor_tensor(
-                out=grouped[:, g, :, :],
-                in0=e_ps[:].rearrange("p t k -> p k t"),
-                in1=be_sb[:, 4 * g : 4 * g + 4].unsqueeze(1).to_broadcast([P, P, 4]),
-                op=ALU.add,
-            )
         b_ps = psum.tile([P, P], BF16, name="b_ps", tag="bank")
         nc.tensor.transpose(b_ps[:], brow[:], ident_bf[:])
         bT = keep.tile([P, P], F32, name="bT")
         nc.vector.tensor_copy(out=bT[:], in_=b_ps[:])
-        ecodes = keep.tile([P, GROUPS * P], U32, name="ecodes", align_bytes=64)
-        eplane = keep.tile([P, GROUPS * P], U8, name="eplane", align_bytes=64)
-        nc.vector.quantize_mx(
-            out=ecodes[:].bitcast(FP8X4),
-            scales=eplane[:],
-            in_=grouped[:].rearrange("p g k t -> p (g k t)"),
-        )
-
-        brz = keep.tile([P, 32], F32, name="brz")
-        nc.vector.tensor_tensor(out=brz[:], in0=bT[:, 0:32], in1=bT[:, 48:80], op=ALU.add)
         bTb = keep.tile([P, P], BF16, name="bTb")
         nc.vector.tensor_copy(out=bTb[:], in_=b_ps[:])
+        brz = keep.tile([P, 32], F32, name="brz")
+        nc.vector.tensor_tensor(out=brz[:], in0=bT[:, 0:32], in1=bT[:, 48:80], op=ALU.add)
 
-        def spread_f32(dst, first):
-            for c in range(NB):
+        def spread_f32(dst, first, banks):
+            for c in banks:
                 bc = psum.tile([P, 4, P], F32, name="bc", tag="bank")
                 for q in range(4):
                     col = first + 4 * c + q
@@ -165,6 +131,49 @@ def tile_encoderrnn_w_kernel(tc, x, w_emb, b_emb, w_ih_words, w_ih_scales, b_ih,
         b_z = keep.tile([P, HID], F32, name="b_z")
         b_in = keep.tile([P, HID], BF16, name="b_in")
         b_hn = keep.tile([P, HID], BF16, name="b_hn")
+
+        x_ps = psum.tile([P, P], BF16, name="x_ps", tag="bank")
+        nc.tensor.transpose(x_ps[:], x_sb[:], perm[:])
+        xT = keep.tile([P, P], BF16, name="xT")
+        nc.vector.tensor_copy(out=xT[:], in_=x_ps[:])
+
+        wT = keep.tile([P, 16, P], BF16, name="wT")
+        for h in range(2):
+            wT_ps = psum.tile([P, 8, P], BF16, name="wT_ps", tag="bank")
+            for q in range(8):
+                nc.tensor.transpose(wT_ps[:, q, :], w_sb[:, 8 * h + q, :], ident_bf[:])
+            if h == 0:
+                nc.vector.tensor_copy(out=wT[:, 0:8, :], in_=wT_ps[:])
+            else:
+                nc.scalar.copy(out=wT[:, 8:16, :], in_=wT_ps[:])
+
+        grouped = keep.tile([P, GROUPS, P, 4], BF16, name="grouped", align_bytes=64)
+
+        def emb_group(g):
+            e_ps = psum.tile([P, 4, P], F32, name="e_ps", tag="bank")
+            for t in range(4):
+                nc.tensor.matmul(e_ps[:, t, :], lhsT=wT[:, 4 * g + t, :], rhs=xT[:], start=True, stop=True)
+            nc.vector.tensor_tensor(
+                out=grouped[:, g, :, :],
+                in0=e_ps[:].rearrange("p t k -> p k t"),
+                in1=be_sb[:, 4 * g : 4 * g + 4].unsqueeze(1).to_broadcast([P, P, 4]),
+                op=ALU.add,
+            )
+
+        spread_f32(b_r, 0, (0, 1))
+        emb_group(0)
+        emb_group(1)
+        spread_f32(b_r, 0, (2, 3))
+        emb_group(2)
+        emb_group(3)
+        spread_bf16(b_hn, 80)
+        ecodes = keep.tile([P, GROUPS * P], U32, name="ecodes", align_bytes=64)
+        eplane = keep.tile([P, GROUPS * P], U8, name="eplane", align_bytes=64)
+        nc.vector.quantize_mx(
+            out=ecodes[:].bitcast(FP8X4),
+            scales=eplane[:],
+            in_=grouped[:].rearrange("p g k t -> p (g k t)"),
+        )
 
         out_h = out_0.rearrange("b s j -> (b s) j")
         out_l = out_1.rearrange("o b j -> (o b) j")
@@ -191,30 +200,36 @@ def tile_encoderrnn_w_kernel(tc, x, w_emb, b_emb, w_ih_words, w_ih_scales, b_ih,
         def cs(c):
             return slice(c * BANK, (c + 1) * BANK)
 
-        spread_f32(b_r, 0)
-        passes(0)
-        spread_bf16(b_hn, 80)
-        passes(1)
-        spread_bf16(b_in, 32)
-        passes(2)
-        passes(3)
-        a_r = {}
         r_t = {}
-        for c in range(NB):
-            a_r[c] = work.tile([P, BANK], F32, name="a")
-            nc.vector.tensor_tensor(out=a_r[c][:], in0=accs[("r", c)][:], in1=b_r[:, cs(c)], op=ALU.add)
-            r_t[c] = work.tile([P, BANK], F32, name="r")
-            nc.scalar.activation(out=r_t[c][:], in_=a_r[c][:], func=ACT.Sigmoid)
-        passes(4)
-        spread_f32(b_z, 16)
         c2 = keep.tile([P, HID], F32, name="c2")
-        for c0 in (0, 2):
+
+        def r_front(c):
+            a = work.tile([P, BANK], F32, name="a")
+            nc.vector.tensor_tensor(out=a[:], in0=accs[("r", c)][:], in1=b_r[:, cs(c)], op=ALU.add)
+            r_t[c] = work.tile([P, BANK], F32, name="r")
+            nc.scalar.activation(out=r_t[c][:], in_=a[:], func=ACT.Sigmoid)
+
+        def r_back(ca, cb):
             c1 = {}
-            for c in (c0, c0 + 1):
+            for c in (ca, cb):
                 c1[c] = work.tile([P, BANK], F32, name="c1")
                 nc.vector.tensor_tensor(out=c1[c][:], in0=r_t[c][:], in1=b_hn[:, cs(c)], op=ALU.mult)
-            for c in (c0, c0 + 1):
+            for c in (ca, cb):
                 nc.vector.tensor_tensor(out=c2[:, cs(c)], in0=c1[c][:], in1=b_in[:, cs(c)], op=ALU.add)
+
+        passes(0)
+        spread_bf16(b_in, 32)
+        passes(1)
+        r_front(0)
+        r_front(1)
+        passes(2)
+        r_back(0, 1)
+        passes(3)
+        r_front(2)
+        r_front(3)
+        passes(4)
+        spread_f32(b_z, 16, (0, 1, 2, 3))
+        r_back(2, 3)
 
         passes(5)
         passes(6)
@@ -242,10 +257,10 @@ def tile_encoderrnn_w_kernel(tc, x, w_emb, b_emb, w_ih_words, w_ih_scales, b_ih,
                 eng.dma_start(out=out_h[r0 : r0 + rows, s0:s1], in_=o_all[p0:p1:ps, s0:s1])
 
         passes(8)
-        z_front(0)
-        z_back(nc.gpsimd, 0)
         passes(9)
+        z_front(0)
         z_front(1)
+        z_back(nc.gpsimd, 0)
         z_back(nc.gpsimd, 1)
         store(nc.sync, BIG_SETS + SMALL_SETS, 0, 1024)
         nc.sync.dma_start(out=out_l[:, 0:1024], in_=o_all[115:128:4, 0:1024])

@@ -80,7 +80,7 @@ def tile_encoderrnn_w_kernel(tc, x, w_emb, b_emb, w_ih_words, w_ih_scales, b_ih,
         nc.vector.memset(planes[:].bitcast(I32), 0)
 
         sc32 = w_ih_scales.bitcast(I32)
-        for q in range(4):
+        for q in (2, 3, 0, 1):
             nc.sync.dma_start(
                 out=planes[32 * q : 32 * q + 16, :].bitcast(I32),
                 in_=sc32[:, 4 * q : 4 * q + 4, :],

@@ -32,9 +32,13 @@ LOADS = [
     ("z", 0, 2, 0, 1024),
     ("z", 2, 2, 0, 1024),
     ("z", 0, 4, 1024, 512),
-    ("z", 0, 3, 1536, 512),
-    ("z", 3, 1, 1536, 512),
+    ("z", 0, 1, 1536, 512),
+    ("z", 1, 1, 1536, 512),
+    ("z", 2, 1, 1536, 512),
+    ("z", 3, 1, 1536, 256),
+    ("z", 3, 1, 1792, 256),
 ]
+Z_UNITS = [(0, 512), (512, 512), (1024, 512), (1536, 256), (1792, 256)]
 BIG_SETS = [(0, 128, 2, 0, 64), (1, 128, 4, 64, 32), (3, 67, 4, 96, 16)]
 SMALL_SETS = [(67, 99, 4, 112, 8), (99, 115, 4, 120, 4)]
 PERM_COPIES = [
@@ -181,18 +185,21 @@ def tile_encoderrnn_w_kernel(tc, x, w_emb, b_emb, w_ih_words, w_ih_scales, b_ih,
 
         def passes(li):
             gate, g0, ng, c0, cols = LOADS[li]
-            for c in range(c0 // BANK, (c0 + cols) // BANK):
+            units = Z_UNITS if gate == "z" else [(c * BANK, BANK) for c in range(NB)]
+            for u0, uw in units:
+                if u0 < c0 or u0 >= c0 + cols:
+                    continue
                 if g0 == 0:
-                    accs[(gate, c)] = psum.tile([P, BANK], F32, name="acc_%s%d" % (gate, c), tag="bank")
+                    accs[(gate, u0)] = psum.tile([P, uw], F32, name="acc_%s%d" % (gate, u0), tag="bank")
                 for gl in range(ng):
                     g = g0 + gl
-                    n0 = GATE_OFF[gate] + c * BANK
+                    n0 = GATE_OFF[gate] + u0
                     nc.tensor.matmul_mx(
-                        out=accs[(gate, c)][:],
+                        out=accs[(gate, u0)][:],
                         lhsT=ecodes[:, g * P : (g + 1) * P].bitcast(FP8X4),
                         lhsT_scale=eplane[:, g * P : (g + 1) * P],
-                        rhs=wtiles[li][:, gl, c * BANK - c0 : (c + 1) * BANK - c0].bitcast(FP8X4),
-                        rhs_scale=planes[4 * g : P, n0 : n0 + BANK],
+                        rhs=wtiles[li][:, gl, u0 - c0 : u0 - c0 + uw].bitcast(FP8X4),
+                        rhs_scale=planes[4 * g : P, n0 : n0 + uw],
                         start=(g == 0),
                         stop=(g == GROUPS - 1),
                     )
@@ -205,7 +212,7 @@ def tile_encoderrnn_w_kernel(tc, x, w_emb, b_emb, w_ih_words, w_ih_scales, b_ih,
 
         def r_front(c):
             a = work.tile([P, BANK], F32, name="a")
-            nc.vector.tensor_tensor(out=a[:], in0=accs[("r", c)][:], in1=b_r[:, cs(c)], op=ALU.add)
+            nc.vector.tensor_tensor(out=a[:], in0=accs[("r", c * BANK)][:], in1=b_r[:, cs(c)], op=ALU.add)
             r_t[c] = work.tile([P, BANK], F32, name="r")
             nc.scalar.activation(out=r_t[c][:], in_=a[:], func=ACT.Sigmoid)
 
@@ -237,20 +244,24 @@ def tile_encoderrnn_w_kernel(tc, x, w_emb, b_emb, w_ih_words, w_ih_scales, b_ih,
         n_all = keep.tile([P, HID], F32, name="n_all")
         for c in range(NB):
             u = work.tile([P, BANK], F32, name="u")
-            nc.vector.tensor_tensor(out=u[:], in0=accs[("n", c)][:], in1=c2[:, cs(c)], op=ALU.add)
+            nc.vector.tensor_tensor(out=u[:], in0=accs[("n", c * BANK)][:], in1=c2[:, cs(c)], op=ALU.add)
             nc.scalar.activation(out=n_all[:, cs(c)], in_=u[:], func=ACT.Tanh)
 
         o_all = keep.tile([P, HID], F32, name="o_all")
         z_t = {}
 
-        def z_front(c):
-            a = work.tile([P, BANK], F32, name="a")
-            nc.vector.tensor_tensor(out=a[:], in0=accs[("z", c)][:], in1=b_z[:, cs(c)], op=ALU.add)
-            z_t[c] = work.tile([P, BANK], F32, name="zc")
-            nc.scalar.activation(out=z_t[c][:], in_=a[:], func=ACT.Sigmoid, scale=-1.0)
+        def z_front(i):
+            u0, uw = Z_UNITS[i]
+            a = work.tile([P, uw], F32, name="a")
+            nc.vector.tensor_tensor(out=a[:], in0=accs[("z", u0)][:], in1=b_z[:, u0 : u0 + uw], op=ALU.add)
+            z_t[i] = work.tile([P, uw], F32, name="zc")
+            nc.scalar.activation(out=z_t[i][:], in_=a[:], func=ACT.Sigmoid, scale=-1.0)
 
-        def z_back(eng, c):
-            eng.tensor_tensor(out=o_all[:, cs(c)], in0=z_t[c][:], in1=n_all[:, cs(c)], op=ALU.mult)
+        def z_back(i, eng):
+            u0, uw = Z_UNITS[i]
+            eng.tensor_tensor(
+                out=o_all[:, u0 : u0 + uw], in0=z_t[i][:], in1=n_all[:, u0 : u0 + uw], op=ALU.mult
+            )
 
         def store(eng, sets, s0, s1):
             for p0, p1, ps, r0, rows in sets:
@@ -260,17 +271,22 @@ def tile_encoderrnn_w_kernel(tc, x, w_emb, b_emb, w_ih_words, w_ih_scales, b_ih,
         passes(9)
         z_front(0)
         z_front(1)
-        z_back(nc.gpsimd, 0)
-        z_back(nc.gpsimd, 1)
+        z_back(0, nc.vector)
+        z_back(1, nc.vector)
         store(nc.sync, BIG_SETS + SMALL_SETS, 0, 1024)
         nc.sync.dma_start(out=out_l[:, 0:1024], in_=o_all[115:128:4, 0:1024])
         passes(10)
         z_front(2)
         passes(11)
         passes(12)
+        z_back(2, nc.gpsimd)
+        passes(13)
+        passes(14)
         z_front(3)
-        z_back(nc.vector, 2)
-        z_back(nc.vector, 3)
+        passes(15)
+        z_front(4)
+        z_back(3, nc.vector)
+        z_back(4, nc.vector)
         store(nc.sync, BIG_SETS, 1024, 2048)
         store(nc.scalar, SMALL_SETS, 1024, 2048)
         nc.scalar.dma_start(out=out_l[:, 1024:2048], in_=o_all[115:128:4, 1024:2048])

@@ -21,10 +21,10 @@ FLOPS = 2 * 128 * 128 * 2048 + 2 * 128 * 2048 * 6144
 
 GATE_OFF = {"r": 0, "z": HID, "n": 2 * HID}
 LOADS = [
-    ("r", 0, 2, 0, 1024),
-    ("r", 2, 2, 0, 1024),
-    ("r", 0, 2, 1024, 1024),
-    ("r", 2, 2, 1024, 1024),
+    ("r", 0, 1, 0, 2048),
+    ("r", 1, 1, 0, 2048),
+    ("r", 2, 1, 0, 2048),
+    ("r", 3, 1, 0, 2048),
     ("n", 0, 1, 0, 2048),
     ("n", 1, 1, 0, 2048),
     ("n", 2, 1, 0, 2048),
@@ -227,15 +227,13 @@ def tile_encoderrnn_w_kernel(tc, x, w_emb, b_emb, w_ih_words, w_ih_scales, b_ih,
         passes(0)
         spread_bf16(b_in, 32)
         passes(1)
-        r_front(0)
-        r_front(1)
         passes(2)
-        r_back(0, 1)
         passes(3)
-        r_front(2)
-        r_front(3)
+        for c in range(NB):
+            r_front(c)
         passes(4)
         spread_f32(b_z, 16, (0, 1, 2, 3))
+        r_back(0, 1)
         r_back(2, 3)
 
         passes(5)

@@ -31,14 +31,12 @@ LOADS = [
     ("n", 3, 1, 0, 2048),
     ("z", 0, 2, 0, 1024),
     ("z", 2, 2, 0, 1024),
-    ("z", 0, 4, 1024, 512),
-    ("z", 0, 1, 1536, 512),
-    ("z", 1, 1, 1536, 512),
-    ("z", 2, 1, 1536, 512),
-    ("z", 3, 1, 1536, 256),
-    ("z", 3, 1, 1792, 256),
+    ("z", 0, 2, 1024, 1024),
+    ("z", 2, 1, 1024, 1024),
+    ("z", 3, 1, 1024, 512),
+    ("z", 3, 1, 1536, 512),
 ]
-Z_UNITS = [(0, 512), (512, 512), (1024, 512), (1536, 256), (1792, 256)]
+Z_UNITS = [(0, 512), (512, 512), (1024, 512), (1536, 512)]
 BIG_SETS = [(0, 128, 2, 0, 64), (1, 128, 4, 64, 32), (3, 67, 4, 96, 16)]
 SMALL_SETS = [(67, 99, 4, 112, 8), (99, 115, 4, 120, 4)]
 PERM_COPIES = [
@@ -274,17 +272,13 @@ def tile_encoderrnn_w_kernel(tc, x, w_emb, b_emb, w_ih_words, w_ih_scales, b_ih,
         store(nc.sync, BIG_SETS + SMALL_SETS, 0, 1024)
         nc.sync.dma_start(out=out_l[:, 0:1024], in_=o_all[115:128:4, 0:1024])
         passes(10)
-        z_front(2)
         passes(11)
         passes(12)
-        z_back(2, nc.gpsimd)
+        z_front(2)
         passes(13)
-        passes(14)
         z_front(3)
-        passes(15)
-        z_front(4)
+        z_back(2, nc.vector)
         z_back(3, nc.vector)
-        z_back(4, nc.vector)
         store(nc.sync, BIG_SETS, 1024, 2048)
         store(nc.scalar, SMALL_SETS, 1024, 2048)
         nc.scalar.dma_start(out=out_l[:, 1024:2048], in_=o_all[115:128:4, 1024:2048])

@@ -17,6 +17,7 @@ HID = 2048
 GROUPS = 4
 BANK = 512
 NB = HID // BANK
+HALF = 3 * HID // 2
 FLOPS = 2 * 128 * 128 * 2048 + 2 * 128 * 2048 * 6144
 
 GATE_OFF = {"r": 0, "z": HID, "n": 2 * HID}
@@ -58,29 +59,24 @@ def tile_encoderrnn_w_kernel(tc, x, w_emb, b_emb, w_ih_words, w_ih_scales, b_ih,
         psum = ctx.enter_context(tc.psum_pool(name="psum", bufs=8))
         ctx.enter_context(tc.manual_schedule())
 
-        be_sb = keep.tile([P, 16], BF16, name="be_sb")
-        nc.scalar.dma_start(
-            out=be_sb[:].rearrange("p (g t) -> p g t", t=4),
-            in_=b_emb.rearrange("(g p t) -> p g t", g=GROUPS, p=P, t=4),
-        )
+        planes = keep.tile([P, 3 * HID], U8, name="planes", align_bytes=64)
+        nc.vector.memset(planes[:, 0:HALF].bitcast(I32), 0)
+        nc.gpsimd.memset(planes[:, HALF:].bitcast(I32), 0)
+        erow = keep.tile([P, BANK], BF16, name="erow")
+        nc.vector.memset(erow[:], 0.0)
         brow = keep.tile([P, P], BF16, name="brow")
         nc.vector.memset(brow[96:128, :], 0.0)
         nc.scalar.dma_start(out=brow[0:48, :], in_=b_ih.rearrange("(r c) -> r c", c=P))
         nc.scalar.dma_start(out=brow[48:96, :], in_=b_hh.rearrange("(r c) -> r c", c=P))
+        nc.scalar.dma_start(out=erow[0:GROUPS, :], in_=b_emb.rearrange("(g c) -> g c", c=BANK))
         x_sb = keep.tile([P, P], BF16, name="x_sb")
         nc.sync.dma_start(out=x_sb[:], in_=x.rearrange("b s i -> (b s) i"))
         w_sb = keep.tile([P, 16, P], BF16, name="w_sb")
-        nc.sync.dma_start(
-            out=w_sb[:].rearrange("p (g t) i -> p g (t i)", t=4),
-            in_=w_emb.rearrange("(g p t) i -> p g (t i)", g=GROUPS, p=P, t=4),
-        )
+        nc.sync.dma_start(out=w_sb[:], in_=w_emb.rearrange("(q s) i -> q s i", s=16))
         warm = keep.tile([P, 1], F32, name="warm")
         nc.vector.memset(warm[:], 0.0)
         warm2 = keep.tile([P, 1], F32, name="warm2")
         nc.scalar.activation(out=warm2[:], in_=warm[:], func=ACT.Sigmoid)
-        planes = keep.tile([P, 3 * HID], U8, name="planes", align_bytes=64)
-        nc.vector.memset(planes[:].bitcast(I32), 0)
-
         sc32 = w_ih_scales.bitcast(I32)
         for q in (2, 3, 0, 1):
             nc.sync.dma_start(
@@ -110,6 +106,11 @@ def tile_encoderrnn_w_kernel(tc, x, w_emb, b_emb, w_ih_words, w_ih_scales, b_ih,
         nc.vector.tensor_copy(out=bT[:], in_=b_ps[:])
         bTb = keep.tile([P, P], BF16, name="bTb")
         nc.vector.tensor_copy(out=bTb[:], in_=b_ps[:])
+        be_ps = psum.tile([P, 4, P], BF16, name="be_ps", tag="bank")
+        for t in range(4):
+            nc.tensor.transpose(be_ps[:, t, :], erow[:, t : BANK : 4], ident_bf[:])
+        be_sb = keep.tile([P, GROUPS, 4], BF16, name="be_sb")
+        nc.vector.tensor_copy(out=be_sb[:], in_=be_ps[:, :, 0:GROUPS].rearrange("p t g -> p g t"))
         brz = keep.tile([P, 32], F32, name="brz")
         nc.vector.tensor_tensor(out=brz[:], in0=bT[:, 0:32], in1=bT[:, 48:80], op=ALU.add)
 
@@ -139,26 +140,28 @@ def tile_encoderrnn_w_kernel(tc, x, w_emb, b_emb, w_ih_words, w_ih_scales, b_ih,
         xT = keep.tile([P, P], BF16, name="xT")
         nc.vector.tensor_copy(out=xT[:], in_=x_ps[:])
 
-        wT = keep.tile([P, 16, P], BF16, name="wT")
-        for h in range(2):
-            wT_ps = psum.tile([P, 8, P], BF16, name="wT_ps", tag="bank")
-            for q in range(8):
-                nc.tensor.transpose(wT_ps[:, q, :], w_sb[:, 8 * h + q, :], ident_bf[:])
-            if h == 0:
-                nc.vector.tensor_copy(out=wT[:, 0:8, :], in_=wT_ps[:])
+        wT = keep.tile([P, 4, GROUPS * P], BF16, name="wT")
+        for half in range(2):
+            wT_ps = psum.tile([P, 2, 4, P], BF16, name="wT_ps", tag="bank")
+            for t in range(2):
+                for h in range(4):
+                    nc.tensor.transpose(wT_ps[:, t, h, :], w_sb[:, 4 * h + 2 * half + t, :], ident_bf[:])
+            wT_out = wT[:, 2 * half : 2 * half + 2, :].rearrange("p t (q h) -> p t q h", h=4)
+            if half == 0:
+                nc.vector.tensor_copy(out=wT_out, in_=wT_ps[:].rearrange("p t h q -> p t q h"))
             else:
-                nc.scalar.copy(out=wT[:, 8:16, :], in_=wT_ps[:])
+                nc.scalar.copy(out=wT_out, in_=wT_ps[:].rearrange("p t h q -> p t q h"))
 
         grouped = keep.tile([P, GROUPS, P, 4], BF16, name="grouped", align_bytes=64)
 
         def emb_group(g):
             e_ps = psum.tile([P, 4, P], F32, name="e_ps", tag="bank")
             for t in range(4):
-                nc.tensor.matmul(e_ps[:, t, :], lhsT=wT[:, 4 * g + t, :], rhs=xT[:], start=True, stop=True)
+                nc.tensor.matmul(e_ps[:, t, :], lhsT=wT[:, t, g * P : (g + 1) * P], rhs=xT[:], start=True, stop=True)
             nc.vector.tensor_tensor(
                 out=grouped[:, g, :, :],
                 in0=e_ps[:].rearrange("p t k -> p k t"),
-                in1=be_sb[:, 4 * g : 4 * g + 4].unsqueeze(1).to_broadcast([P, P, 4]),
+                in1=be_sb[:, g, :].unsqueeze(1).to_broadcast([P, P, 4]),
                 op=ALU.add,
             )
 

@@ -64,10 +64,11 @@ def tile_encoderrnn_w_kernel(tc, x, w_emb, b_emb, w_ih_words, w_ih_scales, b_ih,
         nc.gpsimd.memset(planes[:, HALF:].bitcast(I32), 0)
         erow = keep.tile([P, BANK], BF16, name="erow")
         nc.vector.memset(erow[:], 0.0)
-        brow = keep.tile([P, P], BF16, name="brow")
-        nc.vector.memset(brow[96:128, :], 0.0)
-        nc.scalar.dma_start(out=brow[0:48, :], in_=b_ih.rearrange("(r c) -> r c", c=P))
-        nc.scalar.dma_start(out=brow[48:96, :], in_=b_hh.rearrange("(r c) -> r c", c=P))
+        brow = keep.tile([P, 3 * P], BF16, name="brow")
+        nc.vector.memset(brow[32:64, :], 0.0)
+        nc.vector.memset(brow[64:128, :], 0.0)
+        nc.scalar.dma_start(out=brow[0:16, :], in_=b_ih.rearrange("(r c) -> r c", c=3 * P))
+        nc.scalar.dma_start(out=brow[16:32, :], in_=b_hh.rearrange("(r c) -> r c", c=3 * P))
         nc.scalar.dma_start(out=erow[0:GROUPS, :], in_=b_emb.rearrange("(g c) -> g c", c=BANK))
         x_sb = keep.tile([P, P], BF16, name="x_sb")
         nc.sync.dma_start(out=x_sb[:], in_=x.rearrange("b s i -> (b s) i"))
@@ -100,19 +101,22 @@ def tile_encoderrnn_w_kernel(tc, x, w_emb, b_emb, w_ih_words, w_ih_scales, b_ih,
         for d0, d1, ds, s0, s1, ss in PERM_COPIES:
             nc.vector.tensor_copy(out=perm[:, d0:d1:ds], in_=ident_bf[:, s0:s1:ss])
 
-        b_ps = psum.tile([P, P], BF16, name="b_ps", tag="bank")
-        nc.tensor.transpose(b_ps[:], brow[:], ident_bf[:])
-        bT = keep.tile([P, P], F32, name="bT")
-        nc.vector.tensor_copy(out=bT[:], in_=b_ps[:])
-        bTb = keep.tile([P, P], BF16, name="bTb")
-        nc.vector.tensor_copy(out=bTb[:], in_=b_ps[:])
+        b_ps = psum.tile([P, 3, P], BF16, name="b_ps", tag="bank")
+        for q in range(3):
+            nc.tensor.transpose(b_ps[:, q, :], brow[:, q * P : (q + 1) * P], ident_bf[:])
+        bT = keep.tile([P, 32, 3], F32, name="bT")
+        nc.vector.tensor_copy(out=bT[:], in_=b_ps[:, :, 0:32].rearrange("p q r -> p r q"))
+        bTb = keep.tile([P, 32, 3], BF16, name="bTb")
+        nc.vector.tensor_copy(out=bTb[:], in_=b_ps[:, :, 0:32].rearrange("p q r -> p r q"))
+        bT_f = bT[:].rearrange("p r q -> p (r q)")
+        bT_b = bTb[:].rearrange("p r q -> p (r q)")
         be_ps = psum.tile([P, 4, P], BF16, name="be_ps", tag="bank")
         for t in range(4):
             nc.tensor.transpose(be_ps[:, t, :], erow[:, t : BANK : 4], ident_bf[:])
         be_sb = keep.tile([P, GROUPS, 4], BF16, name="be_sb")
         nc.vector.tensor_copy(out=be_sb[:], in_=be_ps[:, :, 0:GROUPS].rearrange("p t g -> p g t"))
         brz = keep.tile([P, 32], F32, name="brz")
-        nc.vector.tensor_tensor(out=brz[:], in0=bT[:, 0:32], in1=bT[:, 48:80], op=ALU.add)
+        nc.vector.tensor_tensor(out=brz[:], in0=bT_f[:, 0:32], in1=bT_f[:, 48:80], op=ALU.add)
 
         def spread_f32(dst, first, banks):
             for c in banks:
@@ -127,7 +131,7 @@ def tile_encoderrnn_w_kernel(tc, x, w_emb, b_emb, w_ih_words, w_ih_scales, b_ih,
                 bc = psum.tile([P, 8, P], BF16, name="bcb", tag="bank")
                 for q in range(8):
                     col = first + 8 * c + q
-                    nc.tensor.transpose(bc[:, q, :], bTb[:, col : col + 1].to_broadcast([P, P]), ident_bf[:])
+                    nc.tensor.transpose(bc[:, q, :], bT_b[:, col : col + 1].to_broadcast([P, P]), ident_bf[:])
                 nc.scalar.copy(out=dst[:, c * 1024 : (c + 1) * 1024], in_=bc[:].rearrange("p q k -> p (q k)"))
 
         b_r = keep.tile([P, HID], F32, name="b_r")

@@ -20,24 +20,20 @@ NB = HID // BANK
 HALF = 3 * HID // 2
 FLOPS = 2 * 128 * 128 * 2048 + 2 * 128 * 2048 * 6144
 
-GATE_OFF = {"r": 0, "z": HID, "n": 2 * HID}
 LOADS = [
-    ("r", 0, 1, 0, 2048),
-    ("r", 1, 1, 0, 2048),
-    ("r", 2, 1, 0, 2048),
-    ("r", 3, 1, 0, 2048),
-    ("n", 0, 1, 0, 2048),
-    ("n", 1, 1, 0, 2048),
-    ("n", 2, 1, 0, 2048),
-    ("n", 3, 1, 0, 2048),
-    ("z", 0, 2, 0, 1024),
-    ("z", 2, 2, 0, 1024),
-    ("z", 0, 2, 1024, 1024),
-    ("z", 2, 1, 1024, 1024),
-    ("z", 3, 1, 1024, 512),
-    ("z", 3, 1, 1536, 512),
+    (0, 3072, 0, 1),
+    (0, 3072, 1, 1),
+    (0, 3072, 2, 1),
+    (0, 3072, 3, 1),
+    (4096, 2048, 0, 1),
+    (4096, 2048, 1, 1),
+    (4096, 2048, 2, 1),
+    (4096, 2048, 3, 1),
+    (3072, 1024, 0, 2),
+    (3072, 1024, 2, 1),
+    (3072, 512, 3, 1),
+    (3584, 512, 3, 1),
 ]
-Z_UNITS = [(0, 512), (512, 512), (1024, 512), (1536, 512)]
 BIG_SETS = [(0, 128, 2, 0, 64), (1, 128, 4, 64, 32), (3, 67, 4, 96, 16)]
 SMALL_SETS = [(67, 99, 4, 112, 8), (99, 115, 4, 120, 4)]
 PERM_COPIES = [
@@ -56,7 +52,8 @@ def tile_encoderrnn_w_kernel(tc, x, w_emb, b_emb, w_ih_words, w_ih_scales, b_ih,
     with ExitStack() as ctx:
         keep = ctx.enter_context(tc.tile_pool(name="keep", bufs=1))
         work = ctx.enter_context(tc.tile_pool(name="work", bufs=4))
-        psum = ctx.enter_context(tc.psum_pool(name="psum", bufs=8))
+        psum = ctx.enter_context(tc.psum_pool(name="psum", bufs=6))
+        psum_s = ctx.enter_context(tc.psum_pool(name="psum_s", bufs=2))
         ctx.enter_context(tc.manual_schedule())
 
         planes = keep.tile([P, 3 * HID], U8, name="planes", align_bytes=64)
@@ -87,9 +84,8 @@ def tile_encoderrnn_w_kernel(tc, x, w_emb, b_emb, w_ih_words, w_ih_scales, b_ih,
 
         w32 = w_ih_words.rearrange("g p n t -> g p (n t)").bitcast(I32)
         wtiles = []
-        for li, (gate, g0, ng, c0, cols) in enumerate(LOADS):
+        for li, (n0, cols, g0, ng) in enumerate(LOADS):
             wt = keep.tile([P, ng, cols], I32, name="w%d" % li, align_bytes=64)
-            n0 = GATE_OFF[gate] + c0
             nc.sync.dma_start(out=wt[:], in_=w32[g0 : g0 + ng, :, n0 : n0 + cols].rearrange("g p n -> p g n"))
             wtiles.append(wt)
 
@@ -118,21 +114,27 @@ def tile_encoderrnn_w_kernel(tc, x, w_emb, b_emb, w_ih_words, w_ih_scales, b_ih,
         brz = keep.tile([P, 32], F32, name="brz")
         nc.vector.tensor_tensor(out=brz[:], in0=bT_f[:, 0:32], in1=bT_f[:, 48:80], op=ALU.add)
 
-        def spread_f32(dst, first, banks):
-            for c in banks:
-                bc = psum.tile([P, 4, P], F32, name="bc", tag="bank")
+        def copy(eng, out, in_):
+            if eng == "v":
+                nc.vector.tensor_copy(out=out, in_=in_)
+            else:
+                nc.scalar.copy(out=out, in_=in_)
+
+        def spread_f32(dst, first, banks, engs):
+            for c, eng in zip(banks, engs):
+                bc = psum_s.tile([P, 4, P], F32, name="bc", tag="spread")
                 for q in range(4):
                     col = first + 4 * c + q
                     nc.tensor.transpose(bc[:, q, :], brz[:, col : col + 1].to_broadcast([P, P]), ident_f[:])
-                nc.scalar.copy(out=dst[:, c * BANK : (c + 1) * BANK], in_=bc[:].rearrange("p q k -> p (q k)"))
+                copy(eng, dst[:, c * BANK : (c + 1) * BANK], bc[:].rearrange("p q k -> p (q k)"))
 
-        def spread_bf16(dst, first):
-            for c in range(2):
-                bc = psum.tile([P, 8, P], BF16, name="bcb", tag="bank")
+        def spread_bf16(dst, first, engs):
+            for c, eng in zip(range(2), engs):
+                bc = psum_s.tile([P, 8, P], BF16, name="bcb", tag="spread")
                 for q in range(8):
                     col = first + 8 * c + q
                     nc.tensor.transpose(bc[:, q, :], bT_b[:, col : col + 1].to_broadcast([P, P]), ident_bf[:])
-                nc.scalar.copy(out=dst[:, c * 1024 : (c + 1) * 1024], in_=bc[:].rearrange("p q k -> p (q k)"))
+                copy(eng, dst[:, c * 1024 : (c + 1) * 1024], bc[:].rearrange("p q k -> p (q k)"))
 
         b_r = keep.tile([P, HID], F32, name="b_r")
         b_z = keep.tile([P, HID], F32, name="b_z")
@@ -169,42 +171,42 @@ def tile_encoderrnn_w_kernel(tc, x, w_emb, b_emb, w_ih_words, w_ih_scales, b_ih,
                 op=ALU.add,
             )
 
-        spread_f32(b_r, 0, (0, 1))
-        emb_group(0)
-        emb_group(1)
-        spread_f32(b_r, 0, (2, 3))
-        emb_group(2)
-        emb_group(3)
-        spread_bf16(b_hn, 80)
         ecodes = keep.tile([P, GROUPS * P], U32, name="ecodes", align_bytes=64)
         eplane = keep.tile([P, GROUPS * P], U8, name="eplane", align_bytes=64)
-        nc.vector.quantize_mx(
-            out=ecodes[:].bitcast(FP8X4),
-            scales=eplane[:],
-            in_=grouped[:].rearrange("p g k t -> p (g k t)"),
-        )
+
+        def quantize_group(g):
+            nc.vector.quantize_mx(
+                out=ecodes[:, g * P : (g + 1) * P].bitcast(FP8X4),
+                scales=eplane[:, g * P : (g + 1) * P],
+                in_=grouped[:, g, :, :].rearrange("p k t -> p (k t)"),
+            )
+
+        emb_group(0)
+        emb_group(1)
+        quantize_group(0)
+        emb_group(2)
+        quantize_group(1)
+        emb_group(3)
+        quantize_group(2)
+        quantize_group(3)
 
         out_h = out_0.rearrange("b s j -> (b s) j")
         out_l = out_1.rearrange("o b j -> (o b) j")
         accs = {}
 
         def passes(li):
-            gate, g0, ng, c0, cols = LOADS[li]
-            units = Z_UNITS if gate == "z" else [(c * BANK, BANK) for c in range(NB)]
-            for u0, uw in units:
-                if u0 < c0 or u0 >= c0 + cols:
-                    continue
+            l0, cols, g0, ng = LOADS[li]
+            for n0 in range(l0, l0 + cols, BANK):
                 if g0 == 0:
-                    accs[(gate, u0)] = psum.tile([P, uw], F32, name="acc_%s%d" % (gate, u0), tag="bank")
+                    accs[n0] = psum.tile([P, BANK], F32, name="acc%d" % n0, tag="bank")
                 for gl in range(ng):
                     g = g0 + gl
-                    n0 = GATE_OFF[gate] + u0
                     nc.tensor.matmul_mx(
-                        out=accs[(gate, u0)][:],
+                        out=accs[n0][:],
                         lhsT=ecodes[:, g * P : (g + 1) * P].bitcast(FP8X4),
                         lhsT_scale=eplane[:, g * P : (g + 1) * P],
-                        rhs=wtiles[li][:, gl, u0 - c0 : u0 - c0 + uw].bitcast(FP8X4),
-                        rhs_scale=planes[4 * g : P, n0 : n0 + uw],
+                        rhs=wtiles[li][:, gl, n0 - l0 : n0 - l0 + BANK].bitcast(FP8X4),
+                        rhs_scale=planes[4 * g : P, n0 : n0 + BANK],
                         start=(g == 0),
                         stop=(g == GROUPS - 1),
                     )
@@ -217,7 +219,7 @@ def tile_encoderrnn_w_kernel(tc, x, w_emb, b_emb, w_ih_words, w_ih_scales, b_ih,
 
         def r_front(c):
             a = work.tile([P, BANK], F32, name="a")
-            nc.vector.tensor_tensor(out=a[:], in0=accs[("r", c * BANK)][:], in1=b_r[:, cs(c)], op=ALU.add)
+            nc.vector.tensor_tensor(out=a[:], in0=accs[c * BANK][:], in1=b_r[:, cs(c)], op=ALU.add)
             r_t[c] = work.tile([P, BANK], F32, name="r")
             nc.scalar.activation(out=r_t[c][:], in_=a[:], func=ACT.Sigmoid)
 
@@ -229,63 +231,64 @@ def tile_encoderrnn_w_kernel(tc, x, w_emb, b_emb, w_ih_words, w_ih_scales, b_ih,
             for c in (ca, cb):
                 nc.vector.tensor_tensor(out=c2[:, cs(c)], in0=c1[c][:], in1=b_in[:, cs(c)], op=ALU.add)
 
+        o_all = keep.tile([P, HID], F32, name="o_all")
+        z_t = {}
+
+        def z_front(i):
+            u0, uw = i * BANK, BANK
+            a = work.tile([P, uw], F32, name="a")
+            nc.vector.tensor_tensor(out=a[:], in0=accs[HID + u0][:], in1=b_z[:, u0 : u0 + uw], op=ALU.add)
+            z_t[i] = work.tile([P, uw], F32, name="zc")
+            nc.scalar.activation(out=z_t[i][:], in_=a[:], func=ACT.Sigmoid, scale=-1.0)
+
+        def z_back(i):
+            u0, uw = i * BANK, BANK
+            nc.vector.tensor_tensor(
+                out=o_all[:, u0 : u0 + uw], in0=z_t[i][:], in1=n_all[:, u0 : u0 + uw], op=ALU.mult
+            )
+
+        spread_bf16(b_hn, 80, "ss")
         passes(0)
-        spread_bf16(b_in, 32)
+        spread_f32(b_r, 0, (0, 1, 2, 3), "vsvs")
         passes(1)
+        spread_bf16(b_in, 32, "vs")
         passes(2)
         passes(3)
         for c in range(NB):
             r_front(c)
-        passes(4)
-        spread_f32(b_z, 16, (0, 1, 2, 3))
+        spread_f32(b_z, 16, (0, 1), "ss")
         r_back(0, 1)
         r_back(2, 3)
+        z_front(0)
+        z_front(1)
 
+        passes(4)
+        spread_f32(b_z, 16, (2, 3), "ss")
         passes(5)
         passes(6)
         passes(7)
         n_all = keep.tile([P, HID], F32, name="n_all")
         for c in range(NB):
             u = work.tile([P, BANK], F32, name="u")
-            nc.vector.tensor_tensor(out=u[:], in0=accs[("n", c * BANK)][:], in1=c2[:, cs(c)], op=ALU.add)
+            nc.vector.tensor_tensor(out=u[:], in0=accs[2 * HID + c * BANK][:], in1=c2[:, cs(c)], op=ALU.add)
             nc.scalar.activation(out=n_all[:, cs(c)], in_=u[:], func=ACT.Tanh)
-
-        o_all = keep.tile([P, HID], F32, name="o_all")
-        z_t = {}
-
-        def z_front(i):
-            u0, uw = Z_UNITS[i]
-            a = work.tile([P, uw], F32, name="a")
-            nc.vector.tensor_tensor(out=a[:], in0=accs[("z", u0)][:], in1=b_z[:, u0 : u0 + uw], op=ALU.add)
-            z_t[i] = work.tile([P, uw], F32, name="zc")
-            nc.scalar.activation(out=z_t[i][:], in_=a[:], func=ACT.Sigmoid, scale=-1.0)
-
-        def z_back(i, eng):
-            u0, uw = Z_UNITS[i]
-            eng.tensor_tensor(
-                out=o_all[:, u0 : u0 + uw], in0=z_t[i][:], in1=n_all[:, u0 : u0 + uw], op=ALU.mult
-            )
 
         def store(eng, sets, s0, s1):
             for p0, p1, ps, r0, rows in sets:
                 eng.dma_start(out=out_h[r0 : r0 + rows, s0:s1], in_=o_all[p0:p1:ps, s0:s1])
 
-        passes(8)
-        passes(9)
-        z_front(0)
-        z_front(1)
-        z_back(0, nc.vector)
-        z_back(1, nc.vector)
+        z_back(0)
+        z_back(1)
         store(nc.sync, BIG_SETS + SMALL_SETS, 0, 1024)
         nc.sync.dma_start(out=out_l[:, 0:1024], in_=o_all[115:128:4, 0:1024])
+        passes(8)
+        passes(9)
         passes(10)
-        passes(11)
-        passes(12)
         z_front(2)
-        passes(13)
+        passes(11)
         z_front(3)
-        z_back(2, nc.vector)
-        z_back(3, nc.vector)
+        z_back(2)
+        z_back(3)
         store(nc.sync, BIG_SETS, 1024, 2048)
         store(nc.scalar, SMALL_SETS, 1024, 2048)
         nc.scalar.dma_start(out=out_l[:, 1024:2048], in_=o_all[115:128:4, 1024:2048])

@@ -56,20 +56,20 @@ def tile_encoderrnn_w_kernel(tc, x, w_emb, b_emb, w_ih_words, w_ih_scales, b_ih,
         psum_s = ctx.enter_context(tc.psum_pool(name="psum_s", bufs=2))
         ctx.enter_context(tc.manual_schedule())
 
-        planes = keep.tile([P, 3 * HID], U8, name="planes", align_bytes=64)
+        planes = keep.tile([P, 3 * HID], U8, name="planes", align_bytes=256)
         nc.vector.memset(planes[:, 0:HALF].bitcast(I32), 0)
         nc.gpsimd.memset(planes[:, HALF:].bitcast(I32), 0)
-        erow = keep.tile([P, BANK], BF16, name="erow")
+        erow = keep.tile([P, BANK], BF16, name="erow", align_bytes=256)
         nc.vector.memset(erow[:], 0.0)
-        brow = keep.tile([P, 3 * P], BF16, name="brow")
+        brow = keep.tile([P, 3 * P], BF16, name="brow", align_bytes=256)
         nc.vector.memset(brow[32:64, :], 0.0)
         nc.vector.memset(brow[64:128, :], 0.0)
         nc.scalar.dma_start(out=brow[0:16, :], in_=b_ih.rearrange("(r c) -> r c", c=3 * P))
         nc.scalar.dma_start(out=brow[16:32, :], in_=b_hh.rearrange("(r c) -> r c", c=3 * P))
         nc.scalar.dma_start(out=erow[0:GROUPS, :], in_=b_emb.rearrange("(g c) -> g c", c=BANK))
-        x_sb = keep.tile([P, P], BF16, name="x_sb")
+        x_sb = keep.tile([P, P], BF16, name="x_sb", align_bytes=256)
         nc.sync.dma_start(out=x_sb[:], in_=x.rearrange("b s i -> (b s) i"))
-        w_sb = keep.tile([P, 16, P], BF16, name="w_sb")
+        w_sb = keep.tile([P, 16, P], BF16, name="w_sb", align_bytes=256)
         nc.sync.dma_start(out=w_sb[:], in_=w_emb.rearrange("(q s) i -> q s i", s=16))
         warm = keep.tile([P, 1], F32, name="warm")
         nc.vector.memset(warm[:], 0.0)
@@ -85,33 +85,33 @@ def tile_encoderrnn_w_kernel(tc, x, w_emb, b_emb, w_ih_words, w_ih_scales, b_ih,
         w32 = w_ih_words.rearrange("g p n t -> g p (n t)").bitcast(I32)
         wtiles = []
         for li, (n0, cols, g0, ng) in enumerate(LOADS):
-            wt = keep.tile([P, ng, cols], I32, name="w%d" % li, align_bytes=64)
+            wt = keep.tile([P, ng, cols], I32, name="w%d" % li, align_bytes=256)
             nc.sync.dma_start(out=wt[:], in_=w32[g0 : g0 + ng, :, n0 : n0 + cols].rearrange("g p n -> p g n"))
             wtiles.append(wt)
 
-        ident_bf = keep.tile([P, P], BF16, name="ident_bf")
+        ident_bf = keep.tile([P, P], BF16, name="ident_bf", align_bytes=256)
         make_identity(nc, ident_bf[:])
-        ident_f = keep.tile([P, P], F32, name="ident_f")
+        ident_f = keep.tile([P, P], F32, name="ident_f", align_bytes=256)
         make_identity(nc, ident_f[:])
-        perm = keep.tile([P, P], BF16, name="perm")
+        perm = keep.tile([P, P], BF16, name="perm", align_bytes=256)
         for d0, d1, ds, s0, s1, ss in PERM_COPIES:
             nc.vector.tensor_copy(out=perm[:, d0:d1:ds], in_=ident_bf[:, s0:s1:ss])
 
         b_ps = psum.tile([P, 3, P], BF16, name="b_ps", tag="bank")
         for q in range(3):
             nc.tensor.transpose(b_ps[:, q, :], brow[:, q * P : (q + 1) * P], ident_bf[:])
-        bT = keep.tile([P, 32, 3], F32, name="bT")
+        bT = keep.tile([P, 32, 3], F32, name="bT", align_bytes=256)
         nc.vector.tensor_copy(out=bT[:], in_=b_ps[:, :, 0:32].rearrange("p q r -> p r q"))
-        bTb = keep.tile([P, 32, 3], BF16, name="bTb")
+        bTb = keep.tile([P, 32, 3], BF16, name="bTb", align_bytes=256)
         nc.vector.tensor_copy(out=bTb[:], in_=b_ps[:, :, 0:32].rearrange("p q r -> p r q"))
         bT_f = bT[:].rearrange("p r q -> p (r q)")
         bT_b = bTb[:].rearrange("p r q -> p (r q)")
         be_ps = psum.tile([P, 4, P], BF16, name="be_ps", tag="bank")
         for t in range(4):
             nc.tensor.transpose(be_ps[:, t, :], erow[:, t : BANK : 4], ident_bf[:])
-        be_sb = keep.tile([P, GROUPS, 4], BF16, name="be_sb")
+        be_sb = keep.tile([P, GROUPS, 4], BF16, name="be_sb", align_bytes=256)
         nc.vector.tensor_copy(out=be_sb[:], in_=be_ps[:, :, 0:GROUPS].rearrange("p t g -> p g t"))
-        brz = keep.tile([P, 32], F32, name="brz")
+        brz = keep.tile([P, 32], F32, name="brz", align_bytes=256)
         nc.vector.tensor_tensor(out=brz[:], in0=bT_f[:, 0:32], in1=bT_f[:, 48:80], op=ALU.add)
 
         def copy(eng, out, in_):
@@ -136,17 +136,17 @@ def tile_encoderrnn_w_kernel(tc, x, w_emb, b_emb, w_ih_words, w_ih_scales, b_ih,
                     nc.tensor.transpose(bc[:, q, :], bT_b[:, col : col + 1].to_broadcast([P, P]), ident_bf[:])
                 copy(eng, dst[:, c * 1024 : (c + 1) * 1024], bc[:].rearrange("p q k -> p (q k)"))
 
-        b_r = keep.tile([P, HID], F32, name="b_r")
-        b_z = keep.tile([P, HID], F32, name="b_z")
-        b_in = keep.tile([P, HID], BF16, name="b_in")
-        b_hn = keep.tile([P, HID], BF16, name="b_hn")
+        b_r = keep.tile([P, HID], F32, name="b_r", align_bytes=256)
+        b_z = keep.tile([P, HID], F32, name="b_z", align_bytes=256)
+        b_in = keep.tile([P, HID], BF16, name="b_in", align_bytes=256)
+        b_hn = keep.tile([P, HID], BF16, name="b_hn", align_bytes=256)
 
         x_ps = psum.tile([P, P], BF16, name="x_ps", tag="bank")
         nc.tensor.transpose(x_ps[:], x_sb[:], perm[:])
-        xT = keep.tile([P, P], BF16, name="xT")
+        xT = keep.tile([P, P], BF16, name="xT", align_bytes=256)
         nc.vector.tensor_copy(out=xT[:], in_=x_ps[:])
 
-        wT = keep.tile([P, 4, GROUPS * P], BF16, name="wT")
+        wT = keep.tile([P, 4, GROUPS * P], BF16, name="wT", align_bytes=256)
         for half in range(2):
             wT_ps = psum.tile([P, 2, 4, P], BF16, name="wT_ps", tag="bank")
             for t in range(2):
@@ -158,7 +158,7 @@ def tile_encoderrnn_w_kernel(tc, x, w_emb, b_emb, w_ih_words, w_ih_scales, b_ih,
             else:
                 nc.scalar.copy(out=wT_out, in_=wT_ps[:].rearrange("p t h q -> p t q h"))
 
-        grouped = keep.tile([P, GROUPS, P, 4], BF16, name="grouped", align_bytes=64)
+        grouped = keep.tile([P, GROUPS, P, 4], BF16, name="grouped", align_bytes=256)
 
         def emb_group(g):
             e_ps = psum.tile([P, 4, P], F32, name="e_ps", tag="bank")
@@ -171,8 +171,8 @@ def tile_encoderrnn_w_kernel(tc, x, w_emb, b_emb, w_ih_words, w_ih_scales, b_ih,
                 op=ALU.add,
             )
 
-        ecodes = keep.tile([P, GROUPS * P], U32, name="ecodes", align_bytes=64)
-        eplane = keep.tile([P, GROUPS * P], U8, name="eplane", align_bytes=64)
+        ecodes = keep.tile([P, GROUPS * P], U32, name="ecodes", align_bytes=256)
+        eplane = keep.tile([P, GROUPS * P], U8, name="eplane", align_bytes=256)
 
         def quantize_group(g):
             nc.vector.quantize_mx(
@@ -215,7 +215,7 @@ def tile_encoderrnn_w_kernel(tc, x, w_emb, b_emb, w_ih_words, w_ih_scales, b_ih,
             return slice(c * BANK, (c + 1) * BANK)
 
         r_t = {}
-        c2 = keep.tile([P, HID], F32, name="c2")
+        c2 = keep.tile([P, HID], F32, name="c2", align_bytes=256)
 
         def r_front(c):
             a = work.tile([P, BANK], F32, name="a")
@@ -231,7 +231,7 @@ def tile_encoderrnn_w_kernel(tc, x, w_emb, b_emb, w_ih_words, w_ih_scales, b_ih,
             for c in (ca, cb):
                 nc.vector.tensor_tensor(out=c2[:, cs(c)], in0=c1[c][:], in1=b_in[:, cs(c)], op=ALU.add)
 
-        o_all = keep.tile([P, HID], F32, name="o_all")
+        o_all = keep.tile([P, HID], F32, name="o_all", align_bytes=256)
         z_t = {}
 
         def z_front(i):
@@ -267,7 +267,7 @@ def tile_encoderrnn_w_kernel(tc, x, w_emb, b_emb, w_ih_words, w_ih_scales, b_ih,
         passes(5)
         passes(6)
         passes(7)
-        n_all = keep.tile([P, HID], F32, name="n_all")
+        n_all = keep.tile([P, HID], F32, name="n_all", align_bytes=256)
         for c in range(NB):
             u = work.tile([P, BANK], F32, name="u")
             nc.vector.tensor_tensor(out=u[:], in0=accs[2 * HID + c * BANK][:], in1=c2[:, cs(c)], op=ALU.add)

@@ -61,11 +61,10 @@ def tile_encoderrnn_w_kernel(tc, x, w_emb, b_emb, w_ih_words, w_ih_scales, b_ih,
         nc.gpsimd.memset(planes[:, HALF:].bitcast(I32), 0)
         erow = keep.tile([P, BANK], BF16, name="erow", align_bytes=256)
         nc.vector.memset(erow[:], 0.0)
-        brow = keep.tile([P, 3 * P], BF16, name="brow", align_bytes=256)
-        nc.vector.memset(brow[32:64, :], 0.0)
-        nc.vector.memset(brow[64:128, :], 0.0)
-        nc.scalar.dma_start(out=brow[0:16, :], in_=b_ih.rearrange("(r c) -> r c", c=3 * P))
-        nc.scalar.dma_start(out=brow[16:32, :], in_=b_hh.rearrange("(r c) -> r c", c=3 * P))
+        brow = keep.tile([P, P], BF16, name="brow", align_bytes=256)
+        nc.vector.memset(brow[96:128, :], 0.0)
+        nc.scalar.dma_start(out=brow[0:48, :], in_=b_ih.rearrange("(r c) -> r c", c=P))
+        nc.scalar.dma_start(out=brow[48:96, :], in_=b_hh.rearrange("(r c) -> r c", c=P))
         nc.scalar.dma_start(out=erow[0:GROUPS, :], in_=b_emb.rearrange("(g c) -> g c", c=BANK))
         x_sb = keep.tile([P, P], BF16, name="x_sb", align_bytes=256)
         nc.sync.dma_start(out=x_sb[:], in_=x.rearrange("b s i -> (b s) i"))
@@ -97,22 +96,19 @@ def tile_encoderrnn_w_kernel(tc, x, w_emb, b_emb, w_ih_words, w_ih_scales, b_ih,
         for d0, d1, ds, s0, s1, ss in PERM_COPIES:
             nc.vector.tensor_copy(out=perm[:, d0:d1:ds], in_=ident_bf[:, s0:s1:ss])
 
-        b_ps = psum.tile([P, 3, P], BF16, name="b_ps", tag="bank")
-        for q in range(3):
-            nc.tensor.transpose(b_ps[:, q, :], brow[:, q * P : (q + 1) * P], ident_bf[:])
-        bT = keep.tile([P, 32, 3], F32, name="bT", align_bytes=256)
-        nc.vector.tensor_copy(out=bT[:], in_=b_ps[:, :, 0:32].rearrange("p q r -> p r q"))
-        bTb = keep.tile([P, 32, 3], BF16, name="bTb", align_bytes=256)
-        nc.vector.tensor_copy(out=bTb[:], in_=b_ps[:, :, 0:32].rearrange("p q r -> p r q"))
-        bT_f = bT[:].rearrange("p r q -> p (r q)")
-        bT_b = bTb[:].rearrange("p r q -> p (r q)")
+        b_ps = psum.tile([P, P], BF16, name="b_ps", tag="bank")
+        nc.tensor.transpose(b_ps[:], brow[:], ident_bf[:])
+        bT = keep.tile([P, P], F32, name="bT", align_bytes=256)
+        nc.vector.tensor_copy(out=bT[:], in_=b_ps[:])
+        bTb = keep.tile([P, P], BF16, name="bTb", align_bytes=256)
+        nc.vector.tensor_copy(out=bTb[:], in_=b_ps[:])
         be_ps = psum.tile([P, 4, P], BF16, name="be_ps", tag="bank")
         for t in range(4):
             nc.tensor.transpose(be_ps[:, t, :], erow[:, t : BANK : 4], ident_bf[:])
         be_sb = keep.tile([P, GROUPS, 4], BF16, name="be_sb", align_bytes=256)
         nc.vector.tensor_copy(out=be_sb[:], in_=be_ps[:, :, 0:GROUPS].rearrange("p t g -> p g t"))
         brz = keep.tile([P, 32], F32, name="brz", align_bytes=256)
-        nc.vector.tensor_tensor(out=brz[:], in0=bT_f[:, 0:32], in1=bT_f[:, 48:80], op=ALU.add)
+        nc.vector.tensor_tensor(out=brz[:], in0=bT[:, 0:32], in1=bT[:, 48:80], op=ALU.add)
 
         def copy(eng, out, in_):
             if eng == "v":
@@ -133,7 +129,7 @@ def tile_encoderrnn_w_kernel(tc, x, w_emb, b_emb, w_ih_words, w_ih_scales, b_ih,
                 bc = psum_s.tile([P, 8, P], BF16, name="bcb", tag="spread")
                 for q in range(8):
                     col = first + 8 * c + q
-                    nc.tensor.transpose(bc[:, q, :], bT_b[:, col : col + 1].to_broadcast([P, P]), ident_bf[:])
+                    nc.tensor.transpose(bc[:, q, :], bTb[:, col : col + 1].to_broadcast([P, P]), ident_bf[:])
                 copy(eng, dst[:, c * 1024 : (c + 1) * 1024], bc[:].rearrange("p q k -> p (q k)"))
 
         b_r = keep.tile([P, HID], F32, name="b_r", align_bytes=256)

@@ -230,17 +230,18 @@ def tile_encoderrnn_w_kernel(tc, x, w_emb, b_emb, w_ih_words, w_ih_scales, b_ih,
         o_all = keep.tile([P, HID], F32, name="o_all", align_bytes=256)
         z_t = {}
 
-        def z_front(i):
-            u0, uw = i * BANK, BANK
+        def z_front(u0, uw):
+            b0 = u0 // BANK * BANK
             a = work.tile([P, uw], F32, name="a")
-            nc.vector.tensor_tensor(out=a[:], in0=accs[HID + u0][:], in1=b_z[:, u0 : u0 + uw], op=ALU.add)
-            z_t[i] = work.tile([P, uw], F32, name="zc")
-            nc.scalar.activation(out=z_t[i][:], in_=a[:], func=ACT.Sigmoid, scale=-1.0)
-
-        def z_back(i):
-            u0, uw = i * BANK, BANK
             nc.vector.tensor_tensor(
-                out=o_all[:, u0 : u0 + uw], in0=z_t[i][:], in1=n_all[:, u0 : u0 + uw], op=ALU.mult
+                out=a[:], in0=accs[HID + b0][:, u0 - b0 : u0 - b0 + uw], in1=b_z[:, u0 : u0 + uw], op=ALU.add
+            )
+            z_t[u0] = work.tile([P, uw], F32, name="zc%d" % u0, bufs=1)
+            nc.scalar.activation(out=z_t[u0][:], in_=a[:], func=ACT.Sigmoid, scale=-1.0)
+
+        def z_back(u0, uw):
+            nc.vector.tensor_tensor(
+                out=o_all[:, u0 : u0 + uw], in0=z_t[u0][:], in1=n_all[:, u0 : u0 + uw], op=ALU.mult
             )
 
         spread_bf16(b_hn, 80, "ss")
@@ -255,8 +256,8 @@ def tile_encoderrnn_w_kernel(tc, x, w_emb, b_emb, w_ih_words, w_ih_scales, b_ih,
         spread_f32(b_z, 16, (0, 1), "ss")
         r_back(0, 1)
         r_back(2, 3)
-        z_front(0)
-        z_front(1)
+        z_front(0, 512)
+        z_front(512, 512)
 
         passes(4)
         spread_f32(b_z, 16, (2, 3), "ss")
@@ -273,18 +274,23 @@ def tile_encoderrnn_w_kernel(tc, x, w_emb, b_emb, w_ih_words, w_ih_scales, b_ih,
             for p0, p1, ps, r0, rows in sets:
                 eng.dma_start(out=out_h[r0 : r0 + rows, s0:s1], in_=o_all[p0:p1:ps, s0:s1])
 
-        z_back(0)
-        z_back(1)
-        store(nc.sync, BIG_SETS + SMALL_SETS, 0, 1024)
-        nc.sync.dma_start(out=out_l[:, 0:1024], in_=o_all[115:128:4, 0:1024])
+        z_back(0, 512)
+        z_back(512, 512)
+        store(nc.sync, BIG_SETS, 0, 1024)
+        store(nc.gpsimd, SMALL_SETS, 0, 1024)
+        nc.gpsimd.dma_start(out=out_l[:, 0:1024], in_=o_all[115:128:4, 0:1024])
         passes(8)
         passes(9)
         passes(10)
-        z_front(2)
+        z_front(1024, 512)
         passes(11)
-        z_front(3)
-        z_back(2)
-        z_back(3)
-        store(nc.sync, BIG_SETS, 1024, 2048)
+        z_front(1536, 256)
+        z_front(1792, 256)
+        z_back(1024, 512)
+        store(nc.sync, BIG_SETS[0:2], 1024, 1536)
+        z_back(1536, 256)
+        z_back(1792, 256)
+        store(nc.sync, BIG_SETS[0:2], 1536, 2048)
+        store(nc.sync, BIG_SETS[2:3], 1024, 2048)
         store(nc.scalar, SMALL_SETS, 1024, 2048)
         nc.scalar.dma_start(out=out_l[:, 1024:2048], in_=o_all[115:128:4, 1024:2048])

from contextlib import ExitStack

import concourse.mybir as mybir
from concourse.masks import make_identity

F32 = mybir.dt.float32
BF16 = mybir.dt.bfloat16
I32 = mybir.dt.int32
U32 = mybir.dt.uint32
U8 = mybir.dt.uint8
FP8X4 = mybir.dt.float8_e4m3fn_x4
ACT = mybir.ActivationFunctionType
ALU = mybir.AluOpType

P = 128
HID = 2048
GROUPS = 4
BANK = 512
NB = HID // BANK
HALF = 3 * HID // 2
FLOPS = 2 * 128 * 128 * 2048 + 2 * 128 * 2048 * 6144

LOADS = [
    (0, 3072, 0, 1),
    (0, 3072, 1, 1),
    (0, 3072, 2, 1),
    (0, 3072, 3, 1),
    (4096, 2048, 0, 1),
    (4096, 2048, 1, 1),
    (4096, 2048, 2, 1),
    (4096, 2048, 3, 1),
    (3072, 1024, 0, 2),
    (3072, 1024, 2, 1),
    (3072, 512, 3, 1),
    (3584, 512, 3, 1),
]
BIG_SETS = [(0, 128, 2, 0, 64), (1, 128, 4, 64, 32), (3, 67, 4, 96, 16)]
SMALL_SETS = [(67, 99, 4, 112, 8), (99, 115, 4, 120, 4)]
PERM_COPIES = [
    (0, 62, 2, 0, 31, 1),
    (62, 124, 2, 32, 63, 1),
    (124, 128, 2, 64, 66, 1),
    (1, 117, 4, 66, 95, 1),
    (117, 128, 4, 96, 99, 1),
    (3, 115, 4, 99, 127, 1),
    (115, 128, 4, 31, 128, 32),
]


def tile_encoderrnn_w_kernel(tc, x, w_emb, b_emb, w_ih_words, w_ih_scales, b_ih, b_hh, out_0, out_1):
    nc = tc.nc
    with ExitStack() as ctx:
        keep = ctx.enter_context(tc.tile_pool(name="keep", bufs=1))
        work = ctx.enter_context(tc.tile_pool(name="work", bufs=4))
        psum = ctx.enter_context(tc.psum_pool(name="psum", bufs=6))
        psum_s = ctx.enter_context(tc.psum_pool(name="psum_s", bufs=2))
        ctx.enter_context(tc.manual_schedule())

        planes = keep.tile([P, 3 * HID], U8, name="planes", align_bytes=256)
        nc.vector.memset(planes[:, 0:HALF].bitcast(I32), 0)
        nc.gpsimd.memset(planes[:, HALF:].bitcast(I32), 0)
        erow = keep.tile([P, BANK], BF16, name="erow", align_bytes=256)
        nc.vector.memset(erow[:], 0.0)
        brow = keep.tile([P, P], BF16, name="brow", align_bytes=256)
        nc.vector.memset(brow[96:128, :], 0.0)
        nc.scalar.dma_start(out=brow[0:48, :], in_=b_ih.rearrange("(r c) -> r c", c=P))
        nc.scalar.dma_start(out=brow[48:96, :], in_=b_hh.rearrange("(r c) -> r c", c=P))
        nc.scalar.dma_start(out=erow[0:GROUPS, :], in_=b_emb.rearrange("(g c) -> g c", c=BANK))
        x_sb = keep.tile([P, P], BF16, name="x_sb", align_bytes=256)
        nc.sync.dma_start(out=x_sb[:], in_=x.rearrange("b s i -> (b s) i"))
        w_sb = keep.tile([P, 16, P], BF16, name="w_sb", align_bytes=256)
        nc.sync.dma_start(out=w_sb[:], in_=w_emb.rearrange("(q s) i -> q s i", s=16))
        warm = keep.tile([P, 1], F32, name="warm")
        nc.vector.memset(warm[:], 0.0)
        warm2 = keep.tile([P, 1], F32, name="warm2")
        nc.scalar.activation(out=warm2[:], in_=warm[:], func=ACT.Sigmoid)
        sc32 = w_ih_scales.bitcast(I32)
        for q in (2, 3, 0, 1):
            nc.sync.dma_start(
                out=planes[32 * q : 32 * q + 16, :].bitcast(I32),
                in_=sc32[:, 4 * q : 4 * q + 4, :],
            )

        w32 = w_ih_words.rearrange("g p n t -> g p (n t)").bitcast(I32)
        wtiles = []
        for li, (n0, cols, g0, ng) in enumerate(LOADS):
            wt = keep.tile([P, ng, cols], I32, name="w%d" % li, align_bytes=256)
            nc.sync.dma_start(out=wt[:], in_=w32[g0 : g0 + ng, :, n0 : n0 + cols].rearrange("g p n -> p g n"))
            wtiles.append(wt)

        ident_bf = keep.tile([P, P], BF16, name="ident_bf", align_bytes=256)
        make_identity(nc, ident_bf[:])
        ident_f = keep.tile([P, P], F32, name="ident_f", align_bytes=256)
        make_identity(nc, ident_f[:])
        perm = keep.tile([P, P], BF16, name="perm", align_bytes=256)
        for d0, d1, ds, s0, s1, ss in PERM_COPIES:
            nc.vector.tensor_copy(out=perm[:, d0:d1:ds], in_=ident_bf[:, s0:s1:ss])

        b_ps = psum.tile([P, P], BF16, name="b_ps", tag="bank")
        nc.tensor.transpose(b_ps[:], brow[:], ident_bf[:])
        bT = keep.tile([P, P], F32, name="bT", align_bytes=256)
        nc.vector.tensor_copy(out=bT[:], in_=b_ps[:])
        bTb = keep.tile([P, P], BF16, name="bTb", align_bytes=256)
        nc.vector.tensor_copy(out=bTb[:], in_=b_ps[:])
        be_ps = psum.tile([P, 4, P], BF16, name="be_ps", tag="bank")
        for t in range(4):
            nc.tensor.transpose(be_ps[:, t, :], erow[:, t : BANK : 4], ident_bf[:])
        be_sb = keep.tile([P, GROUPS, 4], BF16, name="be_sb", align_bytes=256)
        nc.vector.tensor_copy(out=be_sb[:], in_=be_ps[:, :, 0:GROUPS].rearrange("p t g -> p g t"))
        brz = keep.tile([P, 32], F32, name="brz", align_bytes=256)
        nc.vector.tensor_tensor(out=brz[:], in0=bT[:, 0:32], in1=bT[:, 48:80], op=ALU.add)

        def copy(eng, out, in_):
            if eng == "v":
                nc.vector.tensor_copy(out=out, in_=in_)
            else:
                nc.scalar.copy(out=out, in_=in_)

        def spread_f32(dst, first, banks, engs):
            for c, eng in zip(banks, engs):
                bc = psum_s.tile([P, 4, P], F32, name="bc", tag="spread")
                for q in range(4):
                    col = first + 4 * c + q
                    nc.tensor.transpose(bc[:, q, :], brz[:, col : col + 1].to_broadcast([P, P]), ident_f[:])
                copy(eng, dst[:, c * BANK : (c + 1) * BANK], bc[:].rearrange("p q k -> p (q k)"))

        def spread_bf16(dst, first, engs):
            for c, eng in zip(range(2), engs):
                bc = psum_s.tile([P, 8, P], BF16, name="bcb", tag="spread")
                for q in range(8):
                    col = first + 8 * c + q
                    nc.tensor.transpose(bc[:, q, :], bTb[:, col : col + 1].to_broadcast([P, P]), ident_bf[:])
                copy(eng, dst[:, c * 1024 : (c + 1) * 1024], bc[:].rearrange("p q k -> p (q k)"))

        b_r = keep.tile([P, HID], F32, name="b_r", align_bytes=256)
        b_z = keep.tile([P, HID], F32, name="b_z", align_bytes=256)
        b_in = keep.tile([P, HID], BF16, name="b_in", align_bytes=256)
        b_hn = keep.tile([P, HID], BF16, name="b_hn", align_bytes=256)

        x_ps = psum.tile([P, P], BF16, name="x_ps", tag="bank")
        nc.tensor.transpose(x_ps[:], x_sb[:], perm[:])
        xT = keep.tile([P, P], BF16, name="xT", align_bytes=256)
        nc.vector.tensor_copy(out=xT[:], in_=x_ps[:])

        wT = keep.tile([P, 4, GROUPS * P], BF16, name="wT", align_bytes=256)
        for half in range(2):
            wT_ps = psum.tile([P, 2, 4, P], BF16, name="wT_ps", tag="bank")
            for t in range(2):
                for h in range(4):
                    nc.tensor.transpose(wT_ps[:, t, h, :], w_sb[:, 4 * h + 2 * half + t, :], ident_bf[:])
            wT_out = wT[:, 2 * half : 2 * half + 2, :].rearrange("p t (q h) -> p t q h", h=4)
            if half == 0:
                nc.vector.tensor_copy(out=wT_out, in_=wT_ps[:].rearrange("p t h q -> p t q h"))
            else:
                nc.scalar.copy(out=wT_out, in_=wT_ps[:].rearrange("p t h q -> p t q h"))

        grouped = keep.tile([P, GROUPS, P, 4], BF16, name="grouped", align_bytes=256)

        def emb_group(g):
            e_ps = psum.tile([P, 4, P], F32, name="e_ps", tag="bank")
            for t in range(4):
                nc.tensor.matmul(e_ps[:, t, :], lhsT=wT[:, t, g * P : (g + 1) * P], rhs=xT[:], start=True, stop=True)
            nc.vector.tensor_tensor(
                out=grouped[:, g, :, :],
                in0=e_ps[:].rearrange("p t k -> p k t"),
                in1=be_sb[:, g, :].unsqueeze(1).to_broadcast([P, P, 4]),
                op=ALU.add,
            )

        ecodes = keep.tile([P, GROUPS * P], U32, name="ecodes", align_bytes=256)
        eplane = keep.tile([P, GROUPS * P], U8, name="eplane", align_bytes=256)

        def quantize_group(g):
            nc.vector.quantize_mx(
                out=ecodes[:, g * P : (g + 1) * P].bitcast(FP8X4),
                scales=eplane[:, g * P : (g + 1) * P],
                in_=grouped[:, g, :, :].rearrange("p k t -> p (k t)"),
            )

        emb_group(0)
        emb_group(1)
        quantize_group(0)
        emb_group(2)
        quantize_group(1)
        emb_group(3)
        quantize_group(2)
        quantize_group(3)

        out_h = out_0.rearrange("b s j -> (b s) j")
        out_l = out_1.rearrange("o b j -> (o b) j")
        accs = {}

        def passes(li):
            l0, cols, g0, ng = LOADS[li]
            for n0 in range(l0, l0 + cols, BANK):
                if g0 == 0:
                    accs[n0] = psum.tile([P, BANK], F32, name="acc%d" % n0, tag="bank")
                for gl in range(ng):
                    g = g0 + gl
                    nc.tensor.matmul_mx(
                        out=accs[n0][:],
                        lhsT=ecodes[:, g * P : (g + 1) * P].bitcast(FP8X4),
                        lhsT_scale=eplane[:, g * P : (g + 1) * P],
                        rhs=wtiles[li][:, gl, n0 - l0 : n0 - l0 + BANK].bitcast(FP8X4),
                        rhs_scale=planes[4 * g : P, n0 : n0 + BANK],
                        start=(g == 0),
                        stop=(g == GROUPS - 1),
                    )

        def cs(c):
            return slice(c * BANK, (c + 1) * BANK)

        r_t = {}
        c2 = keep.tile([P, HID], F32, name="c2", align_bytes=256)

        def r_front(c):
            a = work.tile([P, BANK], F32, name="a")
            nc.vector.tensor_tensor(out=a[:], in0=accs[c * BANK][:], in1=b_r[:, cs(c)], op=ALU.add)
            r_t[c] = work.tile([P, BANK], F32, name="r")
            nc.scalar.activation(out=r_t[c][:], in_=a[:], func=ACT.Sigmoid)

        def r_back(ca, cb):
            c1 = {}
            for c in (ca, cb):
                c1[c] = work.tile([P, BANK], F32, name="c1")
                nc.vector.tensor_tensor(out=c1[c][:], in0=r_t[c][:], in1=b_hn[:, cs(c)], op=ALU.mult)
            for c in (ca, cb):
                nc.vector.tensor_tensor(out=c2[:, cs(c)], in0=c1[c][:], in1=b_in[:, cs(c)], op=ALU.add)

        o_all = keep.tile([P, HID], F32, name="o_all", align_bytes=256)
        z_t = {}

        def z_front(u0, uw):
            b0 = u0 // BANK * BANK
            a = work.tile([P, uw], F32, name="a")
            nc.vector.tensor_tensor(
                out=a[:], in0=accs[HID + b0][:, u0 - b0 : u0 - b0 + uw], in1=b_z[:, u0 : u0 + uw], op=ALU.add
            )
            z_t[u0] = work.tile([P, uw], F32, name="zc%d" % u0, bufs=1)
            nc.scalar.activation(out=z_t[u0][:], in_=a[:], func=ACT.Sigmoid, scale=-1.0)

        def z_back(u0, uw):
            nc.vector.tensor_tensor(
                out=o_all[:, u0 : u0 + uw], in0=z_t[u0][:], in1=n_all[:, u0 : u0 + uw], op=ALU.mult
            )

        spread_bf16(b_hn, 80, "ss")
        passes(0)
        spread_f32(b_r, 0, (0, 1, 2, 3), "vsvs")
        passes(1)
        spread_bf16(b_in, 32, "vs")
        passes(2)
        passes(3)
        for c in range(NB):
            r_front(c)
        spread_f32(b_z, 16, (0, 1), "ss")
        r_back(0, 1)
        r_back(2, 3)
        z_front(0, 512)
        z_front(512, 512)

        passes(4)
        spread_f32(b_z, 16, (2, 3), "ss")
        passes(5)
        passes(6)
        passes(7)
        n_all = keep.tile([P, HID], F32, name="n_all", align_bytes=256)
        for c in range(NB):
            u = work.tile([P, BANK], F32, name="u")
            nc.vector.tensor_tensor(out=u[:], in0=accs[2 * HID + c * BANK][:], in1=c2[:, cs(c)], op=ALU.add)
            nc.scalar.activation(out=n_all[:, cs(c)], in_=u[:], func=ACT.Tanh)

        def store(eng, sets, s0, s1):
            for p0, p1, ps, r0, rows in sets:
                eng.dma_start(out=out_h[r0 : r0 + rows, s0:s1], in_=o_all[p0:p1:ps, s0:s1])

        z_back(0, 512)
        z_back(512, 512)
        store(nc.sync, BIG_SETS, 0, 1024)
        store(nc.gpsimd, SMALL_SETS, 0, 1024)
        nc.gpsimd.dma_start(out=out_l[:, 0:1024], in_=o_all[115:128:4, 0:1024])
        passes(8)
        passes(9)
        passes(10)
        z_front(1024, 512)
        passes(11)
        z_front(1536, 256)
        z_front(1792, 256)
        z_back(1024, 512)
        store(nc.sync, BIG_SETS[0:2], 1024, 1536)
        z_back(1536, 256)
        z_back(1792, 256)
        store(nc.sync, BIG_SETS[0:2], 1536, 2048)
        store(nc.sync, BIG_SETS[2:3], 1024, 2048)
        store(nc.scalar, SMALL_SETS, 1024, 2048)
        nc.scalar.dma_start(out=out_l[:, 1024:2048], in_=o_all[115:128:4, 1024:2048])
